import numpy as np
import ml_dtypes


def mxq(x, axis, fmt="e4m3"):
    dtype, down = {"e4m3": (ml_dtypes.float8_e4m3fn, 7), "e5m2": (ml_dtypes.float8_e5m2, 14)}[fmt]
    v = np.moveaxis(np.asarray(x, np.float32).astype(ml_dtypes.bfloat16).astype(np.float64), axis, -1)
    blocks = v.reshape(v.shape[:-1] + (-1, 32))
    amax = np.abs(blocks).max(-1, keepdims=True)
    byte = np.maximum(np.where(amax > 0, np.frexp(amax)[1] - 1 + 127, 0) - down, 1)
    scale = np.exp2(byte - 127.0)
    codes = (blocks / scale).astype(np.float32).astype(dtype).astype(np.float64)
    return np.moveaxis((codes * scale).reshape(v.shape), -1, axis)


WIDE = False


def mx_kscale(k):
    if not WIDE:
        return np.ones(k)
    levels = np.array([10, -10, 5, -5, 0])
    a = np.random.permutation(np.resize(levels, k // 512 * 4)).reshape(k // 512, 4)
    idx = np.arange(k)
    return np.exp2(a[idx // 512, idx % 128 // 32])


BF16 = ml_dtypes.bfloat16


def bf(x):
    return np.asarray(x, np.float32).astype(BF16)


def f64(x):
    return np.asarray(x).astype(np.float64)


B, H, FEAT, AUX, NS, FC, C = 4096, 512, 128, 128, 2, 1024, 256
IN = FEAT + AUX + NS


def sigmoid(v):
    return 1.0 / (1.0 + np.exp(-v))


def setup_inputs():
    s = mx_kscale(H)
    s = s / s.max()
    col = np.concatenate([np.full(FEAT, 0.6 / np.sqrt(FEAT)), np.full(AUX, 0.6 / np.sqrt(AUX)), np.full(NS, 0.6 / np.sqrt(NS))])
    return {"x": bf(np.random.standard_normal((B, NS))),
            "feat": bf(np.random.standard_normal((B, FEAT))),
            "aux1": bf(np.random.standard_normal((B, AUX))),
            "h": bf(np.random.standard_normal((B, H)) * s),
            "w_ih": bf(np.random.standard_normal((3 * H, IN)) * col),
            "w_hh": bf(np.random.standard_normal((3 * H, H)) / np.sqrt(H) / s),
            "b_ih": bf(np.random.standard_normal(3 * H) * 0.3),
            "b_hh": bf(np.random.standard_normal(3 * H) * 0.3)}


def reference(x, feat, aux1, h, w_ih, w_hh, b_ih, b_hh):
    hh, wi, xx = f64(h), f64(w_ih), f64(x)
    gi = f64(feat) @ wi[:, :FEAT].T + f64(aux1) @ wi[:, FEAT:FEAT + AUX].T
    for j in range(NS):
        gi = gi + xx[:, j:j + 1] * wi[:, FEAT + AUX + j][None, :]
    gi = gi + f64(b_ih)
    gh = (mxq(hh, 1, "e4m3") @ mxq(f64(w_hh), 1, "e4m3").T) + f64(b_hh)
    i_r, i_z, i_n = np.split(gi, 3, axis=1)
    h_r, h_z, h_n = np.split(gh, 3, axis=1)
    r = sigmoid(i_r + h_r)
    z = sigmoid(i_z + h_z)
    n = np.tanh(i_n + r * h_n)
    return (1.0 - z) * n + z * hh

@@ -1,0 +1,314 @@
+from contextlib import ExitStack
+
+import concourse.mybir as mybir
+from concourse.masks import make_identity
+
+F32 = mybir.dt.float32
+BF16 = mybir.dt.bfloat16
+U32 = mybir.dt.uint32
+U8 = mybir.dt.uint8
+FP8X4 = mybir.dt.float8_e4m3fn_x4
+ALU = mybir.AluOpType
+ACT = mybir.ActivationFunctionType
+
+P = 128
+B = 4096
+H = 512
+IN = 258
+BB = 512
+NBLK = B // BB
+NUNIT = NBLK * 4
+NPAIR = NUNIT // 2
+WROW = 528
+FLOPS = 2 * B * 3 * H * (H + IN)
+PIN = True
+ACC = True
+OUT_LAG = 4
+
+
+def tile_wavernncell_pa_t_kernel(tc, x, feat, aux1, h, w_ih, w_hh, b_ih, b_hh, out):
+    nc = tc.nc
+    with ExitStack() as ctx:
+        const = ctx.enter_context(tc.tile_pool(name="const", bufs=1))
+        ld = ctx.enter_context(tc.tile_pool(name="ld", bufs=3))
+        stage = ctx.enter_context(tc.tile_pool(name="stage", bufs=2))
+        ew = ctx.enter_context(tc.tile_pool(name="ew", bufs=2))
+        outp = ctx.enter_context(tc.tile_pool(name="outp", bufs=3))
+        psum = ctx.enter_context(tc.psum_pool(name="psum", bufs=3))
+        if PIN:
+            ctx.enter_context(tc.manual_schedule())
+
+        xf = x.rearrange("b i -> (b i)")
+        whh_v = w_hh.rearrange("(g u m e) k -> m g u (e k)", g=3, u=2, m=P, e=2)
+        wih_v = w_ih.rearrange("(g u m e) k -> m g u (e k)", g=3, u=2, m=P, e=2)
+
+        warm = const.tile([P, 1], F32, name="warm")
+        nc.vector.memset(warm[:], 0.0)
+        nc.scalar.activation(out=warm[:], in_=warm[:], func=ACT.Sigmoid)
+        ident_f = const.tile([P, P], F32, name="ident_f")
+        make_identity(nc, ident_f[:])
+        ident_b = const.tile([P, P], BF16, name="ident_b")
+        make_identity(nc, ident_b[:])
+        brow = const.tile([P, 256], BF16, name="brow")
+        nc.vector.memset(brow[:], 0.0)
+        t4 = const.tile([P, 4, P], BF16, name="t4")
+        nc.vector.memset(t4[:], 0.0)
+        xm = const.tile([P, 2 * B], BF16, name="xm")
+        nc.vector.memset(xm[:], 0.0)
+
+        whh_sb = const.tile([P, 3, 2, 1024], BF16, name="whh_sb")
+        wih_sb = const.tile([P, 3, 2, WROW], BF16, name="wih_sb")
+        wgrp = const.tile([P, 12 * 512], BF16, name="wgrp", align_bytes=64)
+        wc = const.tile([P, 12 * P], U32, name="wc", align_bytes=64)
+        wsc = const.tile([P, 12 * P], U8, name="wsc", align_bytes=64)
+        wiht = const.tile([P, 2, 12, P], BF16, name="wiht")
+        wx = const.tile([P, 3, 2, 2, 2], F32, name="wx")
+        xw = const.tile([P, 4, P], BF16, name="xw")
+        bias = const.tile([P, 24], F32, name="bias")
+        brz = const.tile([P, 8], F32, name="brz")
+
+        whh_w = whh_sb[:].bitcast(F32)
+        wih_w = wih_sb[:].bitcast(F32)
+        wih5 = wih_sb[:, :, :, 0:516].rearrange("m g u (e k) -> m g u e k", e=2)
+        wgrp_w = wgrp[:].bitcast(F32)
+        xmv = xm[:].rearrange("p (b i) -> p b i", i=2)
+
+        loaded = {}
+        staged = {}
+        tags = ["tp", "gi", "gh"]
+        turn = [0]
+
+        def any_bank(shape, dtype):
+            turn[0] += 1
+            return psum.tile(shape, dtype, tag=tags[turn[0] % 3], name="ps_pro", bufs=(2 if turn[0] % 3 == 0 else 3))
+
+        def load(blk):
+            h_sb = ld.tile([P, 4, H], BF16, tag="h", name="h_sb")
+            nc.sync.dma_start(out=h_sb[:], in_=h[blk * BB:(blk + 1) * BB, :].rearrange("(s p) k -> p s k", p=P))
+            cat = ld.tile([P, 4, 256], BF16, tag="cat", name="cat")
+            nc.sync.dma_start(out=cat[:, :, 0:128], in_=feat[blk * BB:(blk + 1) * BB, :].rearrange("(s p) k -> p s k", p=P))
+            nc.sync.dma_start(out=cat[:, :, 128:256], in_=aux1[blk * BB:(blk + 1) * BB, :].rearrange("(s p) k -> p s k", p=P))
+            xb = ld.tile([P, 2 * BB], BF16, tag="xb", name="xb")
+            nc.sync.dma_start(out=xb[:], in_=xf[blk * 2 * BB:(blk + 1) * 2 * BB].partition_broadcast(P))
+            loaded[blk] = (h_sb, cat, xb)
+
+        def stage_h_t(blk, half, ps):
+            if half == 0:
+                hgrp = stage.tile([P, 4 * BB], BF16, tag="hgrp", name="hgrp", bufs=3, align_bytes=64)
+                staged[blk] = [hgrp, None, None, None]
+            hw = loaded[blk][0][:].bitcast(F32)
+            for s2 in range(2):
+                for uu in range(2):
+                    nc.tensor.transpose(ps[:, uu, s2, :], hw[:, half * 2 + s2, uu * P:(uu + 1) * P], ident_f[:])
+
+        def stage_h_c(blk, half, ps):
+            dst = staged[blk][0][:].bitcast(F32)[:, half * 512:(half + 1) * 512].rearrange("p (b u) -> p b u", u=2)
+            nc.scalar.copy(out=dst, in_=ps[:].rearrange("p u s b -> p (s b) u"))
+
+        def stage_cat_t(blk, ps):
+            cw = loaded[blk][1][:].bitcast(F32)
+            for s in range(4):
+                nc.tensor.transpose(ps[:, s // 2, s % 2, :], cw[:, s, :], ident_f[:])
+
+        def stage_cat_c(blk, ps):
+            catt = stage.tile([P, BB], F32, tag="catt", name="catt")
+            nc.scalar.copy(out=catt[:], in_=ps[:].rearrange("p a s b -> p (a s b)"))
+            staged[blk][3] = catt
+
+        def stage_q(blk):
+            hc = stage.tile([P, BB], U32, tag="hc", name="hc", align_bytes=64)
+            hs = stage.tile([P, BB], U8, tag="hs", name="hs", align_bytes=64)
+            nc.vector.quantize_mx(out=hc[:].bitcast(FP8X4), scales=hs[:], in_=staged[blk][0][:])
+            staged[blk][1] = hc
+            staged[blk][2] = hs
+
+        def quant_w(gu):
+            nc.vector.quantize_mx(
+                out=wc[:, gu * 256:(gu + 1) * 256].bitcast(FP8X4),
+                scales=wsc[:, gu * 256:(gu + 1) * 256],
+                in_=wgrp[:, gu * 1024:(gu + 1) * 1024],
+            )
+
+        def prep_w(u):
+            for g in range(3):
+                gu = g * 2 + u
+                ps = any_bank([P, 2, 2, P], F32)
+                for e in range(2):
+                    for uu in range(2):
+                        lo = e * 256 + uu * P
+                        nc.tensor.transpose(ps[:, uu, e, :], whh_w[:, g, u, lo:lo + P], ident_f[:])
+                dst = wgrp_w[:, gu * 512:(gu + 1) * 512].rearrange("p (e m k) -> p e m k", e=2, k=2)
+                nc.vector.tensor_copy(out=dst, in_=ps[:].rearrange("p k e m -> p e m k"))
+                if g > 0:
+                    quant_w(gu - 2)
+            for g in range(3):
+                gu = g * 2 + u
+                ps2 = any_bank([P, 2, P], F32)
+                for e in range(2):
+                    nc.tensor.transpose(ps2[:, e, :], wih_w[:, g, u, e * 129:e * 129 + P], ident_f[:])
+                src = ps2[:].bitcast(BF16).rearrange("w e (m k) -> w k e m", k=2)
+                nc.scalar.copy(out=wiht[:, :, gu * 2:gu * 2 + 2, :], in_=src)
+            quant_w(4 + u)
+            nc.vector.tensor_copy(out=wx[:, :, u, :, :], in_=wih5[:, :, u, :, 256:258])
+            nc.vector.tensor_copy(out=t4[:, u * 2:u * 2 + 2, 0:2], in_=wih5[:, 2, u, :, 256:258])
+
+        nc.sync.dma_start(out=whh_sb[:, :, 0, :], in_=whh_v[:, :, 0, :])
+        nc.sync.dma_start(out=wih_sb[:, :, 0, 0:516], in_=wih_v[:, :, 0, :])
+        nc.sync.dma_start(out=whh_sb[:, :, 1, :], in_=whh_v[:, :, 1, :])
+        nc.sync.dma_start(out=wih_sb[:, :, 1, 0:516], in_=wih_v[:, :, 1, :])
+        load(0)
+        nc.sync.dma_start(out=brow[0:6, :], in_=b_ih.rearrange("(r c) -> r c", c=256))
+        nc.sync.dma_start(out=brow[6:12, :], in_=b_hh.rearrange("(r c) -> r c", c=256))
+        nc.sync.dma_start(out=xm[0:1, :], in_=xf.unsqueeze(0))
+        nc.sync.dma_start(out=xm[1:2, 0:2 * B - 1], in_=xf[1:2 * B].unsqueeze(0))
+        load(1)
+
+        prep_w(0)
+        prep_w(1)
+        psx = any_bank([P, 4, P], BF16)
+        for c in range(4):
+            nc.tensor.transpose(psx[:, c, :], t4[:, c, :], ident_b[:])
+        nc.vector.tensor_copy(out=xw[:], in_=psx[:])
+        for half in range(2):
+            ps = any_bank([P, 2, 2, P], F32)
+            stage_h_t(0, half, ps)
+            stage_h_c(0, half, ps)
+        ps = any_bank([P, 2, 2, P], F32)
+        stage_cat_t(0, ps)
+        stage_cat_c(0, ps)
+        psb = any_bank([P, P], F32)
+        nc.tensor.transpose(psb[:], brow[:].bitcast(F32), ident_f[:])
+        nc.vector.tensor_copy(out=bias[:], in_=psb[:].bitcast(BF16)[:, 0:24])
+        nc.vector.tensor_tensor(out=brz[:], in0=bias[:, 0:8], in1=bias[:, 12:20], op=ALU.add)
+        stage_q(0)
+
+        pairs = {}
+
+        def matmuls(i):
+            blk, c = divmod(i, 4)
+            hc, hs, catt = staged[blk][1], staged[blk][2], staged[blk][3]
+            cb = catt[:].bitcast(BF16).rearrange("p (b e) -> p b e", e=2)
+            res = []
+            for g in range(3):
+                q = g * 4 + c
+                gh = psum.tile([P, BB], F32, tag="gh", name="gh")
+                nc.tensor.matmul_mx(
+                    out=gh[:],
+                    lhsT=wc[:, q * P:(q + 1) * P].bitcast(FP8X4),
+                    lhsT_scale=wsc[:, q * P:(q + 1) * P],
+                    rhs=hc[:].bitcast(FP8X4),
+                    rhs_scale=hs[:],
+                    start=True,
+                    stop=True,
+                )
+                gi = psum.tile([P, BB], F32, tag="gi", name="gi")
+                nc.tensor.matmul(gi[:], lhsT=wiht[:, 0, q, :], rhs=cb[:, :, 0], start=True, stop=False)
+                nc.tensor.matmul(gi[:], lhsT=wiht[:, 1, q, :], rhs=cb[:, :, 1], start=False, stop=(g < 2))
+                if g == 2:
+                    nc.tensor.matmul(gi[:], lhsT=xw[:, c, :], rhs=xmv[:, blk * BB:(blk + 1) * BB, 0], start=False, stop=True)
+                res.append((gi, gh))
+            return res
+
+        def x_terms(i, g, gi, gh, o1, o2):
+            blk, c = divmod(i, 4)
+            u, e = divmod(c, 2)
+            xbv = loaded[blk][2][:].rearrange("p (b i) -> p b i", i=2)
+            nc.vector.scalar_tensor_tensor(out=o2, in0=xbv[:, :, 1], scalar=wx[:, g, u, e, 1:2], in1=gh[:], op0=ALU.mult, op1=ALU.add)
+            nc.vector.scalar_tensor_tensor(out=o1, in0=xbv[:, :, 0], scalar=wx[:, g, u, e, 0:1], in1=gi[:], op0=ALU.mult, op1=ALU.add)
+
+        def out_t(k, ps):
+            w, sp = divmod(k, 2)
+            dd, nn = pairs[w]["d"], pairs[w]["n"]
+            for s2 in range(2):
+                for e in range(2):
+                    lo = (2 * sp + s2) * P
+                    if ACC:
+                        nc.tensor.matmul(ps[:, s2, e, :], lhsT=dd[:, e, lo:lo + P], rhs=ident_f[:], is_transpose=True, start=True, stop=False)
+                        nc.tensor.matmul(ps[:, s2, e, :], lhsT=nn[:, e, lo:lo + P], rhs=ident_f[:], is_transpose=True, start=False, stop=True)
+                    else:
+                        nc.tensor.transpose(ps[:, s2, e, :], dd[:, e, lo:lo + P], ident_f[:])
+
+        def out_c(k, ps, on_vector):
+            w, sp = divmod(k, 2)
+            blk, u = divmod(w, 2)
+            ob = outp.tile([P, 2, 256], F32, tag="ob", name="ob")
+            dst = ob[:].rearrange("b s (p e) -> b s p e", e=2)
+            src = ps[:].rearrange("b s e p -> b s p e")
+            if on_vector:
+                nc.vector.tensor_copy(out=dst, in_=src)
+            else:
+                nc.scalar.copy(out=dst, in_=src)
+            r0 = blk * BB + sp * 256
+            nc.sync.dma_start(out=out[r0:r0 + 256, u * 256:(u + 1) * 256].rearrange("(s b) j -> b s j", b=P), in_=ob[:])
+
+        for i in range(NUNIT + OUT_LAG):
+            blk, c = divmod(i, 4)
+            u, e = divmod(c, 2)
+            w = i // 2
+            live = i < NUNIT
+            nxt = blk + 1
+            k = i - OUT_LAG
+            if live:
+                if c == 0 and blk + 2 < NBLK:
+                    load(blk + 2)
+                (gi_r, gh_r), (gi_z, gh_z), (gi_n, gh_n) = matmuls(i)
+            ps_o = None
+            if 0 <= k:
+                ps_o = psum.tile([P, 2, 2, P], F32, tag="tp", name="ps_o", bufs=2)
+                out_t(k, ps_o)
+            ps_i = None
+            if live and nxt < NBLK and c < 3:
+                ps_i = psum.tile([P, 2, 2, P], F32, tag="tp", name="ps_i", bufs=2)
+                if c < 2:
+                    stage_h_t(nxt, c, ps_i)
+                else:
+                    stage_cat_t(nxt, ps_i)
+            if live:
+                if e == 0:
+                    pairs[w] = {
+                        "a1": ew.tile([P, 2, BB], F32, tag="az1", name="az1"),
+                        "a2": ew.tile([P, 2, BB], F32, tag="az2", name="az2"),
+                        "n": ew.tile([P, 2, BB], F32, tag="n", name="n", bufs=3),
+                    }
+                pw = pairs[w]
+                a1 = ew.tile([P, BB], F32, tag="a1", name="a1")
+                a2 = ew.tile([P, BB], F32, tag="a2", name="a2")
+                x_terms(i, 0, gi_r, gh_r, a1[:], a2[:])
+                nc.vector.tensor_tensor(out=a1[:], in0=a1[:], in1=a2[:], op=ALU.add)
+                r = ew.tile([P, BB], F32, tag="r", name="r")
+                nc.scalar.activation(out=r[:], in_=a1[:], func=ACT.Sigmoid, bias=brz[:, c:c + 1], scale=1.0)
+            if i % 2 == 0 and 2 <= i <= NUNIT:
+                wp = w - 1
+                pp = pairs[wp]
+                up = wp % 2
+                z = ew.tile([P, 2, BB], F32, tag="z", name="z")
+                for ez in range(2):
+                    cz = 4 + 2 * up + ez
+                    nc.scalar.activation(out=z[:, ez, :], in_=pp["a1"][:, ez, :], func=ACT.Sigmoid, bias=brz[:, cz:cz + 1], scale=1.0)
+                eng = nc.vector if wp == NPAIR - 1 else nc.gpsimd
+                eng.tensor_tensor(out=pp["d"][:], in0=pp["d"][:], in1=z[:], op=ALU.mult)
+                if not ACC:
+                    eng.tensor_tensor(out=pp["d"][:], in0=pp["d"][:], in1=pp["n"][:], op=ALU.add)
+            if live:
+                x_terms(i, 1, gi_z, gh_z, pw["a1"][:, e, :], pw["a2"][:, e, :])
+                if e == 1:
+                    nc.gpsimd.tensor_tensor(out=pw["a1"][:], in0=pw["a1"][:], in1=pw["a2"][:], op=ALU.add)
+            if ps_i is not None:
+                if c < 2:
+                    stage_h_c(nxt, c, ps_i)
+                else:
+                    stage_cat_c(nxt, ps_i)
+            if ps_o is not None:
+                out_c(k, ps_o, (not live) and k % 2 == 1)
+            if live:
+                v = ew.tile([P, BB], F32, tag="v", name="v")
+                nc.vector.scalar_tensor_tensor(out=v[:], in0=gh_n[:], scalar=bias[:, 20 + c:21 + c], in1=r[:], op0=ALU.add, op1=ALU.mult)
+                nc.vector.tensor_tensor(out=v[:], in0=gi_n[:], in1=v[:], op=ALU.add)
+                nc.scalar.activation(out=pw["n"][:, e, :], in_=v[:], func=ACT.Tanh, bias=bias[:, 8 + c:9 + c], scale=1.0)
+                if c == 2 and nxt < NBLK:
+                    stage_q(nxt)
+                if e == 1:
+                    pw["d"] = ew.tile([P, 2, BB], F32, tag="d", name="d", bufs=3)
+                    ht = staged[blk][0][:].rearrange("p (b t) -> p t b", t=4)[:, 2 * u:2 * u + 2, :]
+                    eng = nc.vector if w == NPAIR - 1 else nc.gpsimd
+                    eng.tensor_tensor(out=pw["d"][:], in0=ht, in1=pw["n"][:], op=ALU.subtract)

@@ -66,6 +66,7 @@ def tile_wavernncell_pa_t_kernel(tc, x, feat, aux1, h, w_ih, w_hh, b_ih, b_hh, o
         xw = const.tile([P, 4, P], BF16, name="xw")
         bias = const.tile([P, 24], F32, name="bias")
         brz = const.tile([P, 8], F32, name="brz")
+        xs = const.tile([P, B // P, 2], BF16, name="xs")
 
         whh_w = whh_sb[:].bitcast(F32)
         wih_w = wih_sb[:].bitcast(F32)
@@ -80,7 +81,7 @@ def tile_wavernncell_pa_t_kernel(tc, x, feat, aux1, h, w_ih, w_hh, b_ih, b_hh, o
 
         def any_bank(shape, dtype):
             turn[0] += 1
-            return psum.tile(shape, dtype, tag=tags[turn[0] % 3], name="ps_pro", bufs=(2 if turn[0] % 3 == 0 else 3))
+            return psum.tile(shape, dtype, tag=tags[turn[0] % 3], name="ps_pro", bufs=(3 if turn[0] % 3 == 2 else 2))
 
         def load(blk):
             h_sb = ld.tile([P, 4, H], BF16, tag="h", name="h_sb")
@@ -114,6 +115,12 @@ def tile_wavernncell_pa_t_kernel(tc, x, feat, aux1, h, w_ih, w_hh, b_ih, b_hh, o
             catt = stage.tile([P, BB], F32, tag="catt", name="catt")
             nc.scalar.copy(out=catt[:], in_=ps[:].rearrange("p a s b -> p (a s b)"))
             staged[blk][3] = catt
+
+        def x1_bank(blk):
+            px = psum.tile([P, BB], BF16, tag="px", name="px", bufs=1)
+            for s in range(4):
+                nc.tensor.transpose(px[:, s * P:(s + 1) * P], xs[:, blk * 4 + s, 1:2].to_broadcast([P, P]), ident_b[:])
+            staged[blk].append(px)
 
         def stage_q(blk):
             hc = stage.tile([P, BB], U32, tag="hc", name="hc", align_bytes=64)
@@ -157,6 +164,7 @@ def tile_wavernncell_pa_t_kernel(tc, x, feat, aux1, h, w_ih, w_hh, b_ih, b_hh, o
         nc.sync.dma_start(out=whh_sb[:, :, 1, :], in_=whh_v[:, :, 1, :])
         nc.sync.dma_start(out=wih_sb[:, :, 1, 0:516], in_=wih_v[:, :, 1, :])
         load(0)
+        nc.sync.dma_start(out=xs[:], in_=x.rearrange("(t p) i -> p t i", p=P))
         nc.sync.dma_start(out=brow[0:6, :], in_=b_ih.rearrange("(r c) -> r c", c=256))
         nc.sync.dma_start(out=brow[6:12, :], in_=b_hh.rearrange("(r c) -> r c", c=256))
         nc.sync.dma_start(out=xm[0:1, :], in_=xf.unsqueeze(0))
@@ -181,6 +189,7 @@ def tile_wavernncell_pa_t_kernel(tc, x, feat, aux1, h, w_ih, w_hh, b_ih, b_hh, o
         nc.vector.tensor_copy(out=bias[:], in_=psb[:].bitcast(BF16)[:, 0:24])
         nc.vector.tensor_tensor(out=brz[:], in0=bias[:, 0:8], in1=bias[:, 12:20], op=ALU.add)
         stage_q(0)
+        x1_bank(0)
 
         pairs = {}
 
@@ -201,7 +210,7 @@ def tile_wavernncell_pa_t_kernel(tc, x, feat, aux1, h, w_ih, w_hh, b_ih, b_hh, o
                     start=True,
                     stop=True,
                 )
-                gi = psum.tile([P, BB], F32, tag="gi", name="gi")
+                gi = psum.tile([P, BB], F32, tag="gi", name="gi", bufs=2)
                 nc.tensor.matmul(gi[:], lhsT=wiht[:, 0, q, :], rhs=cb[:, :, 0], start=True, stop=False)
                 nc.tensor.matmul(gi[:], lhsT=wiht[:, 1, q, :], rhs=cb[:, :, 1], start=False, stop=(g < 2))
                 if g == 2:
@@ -272,9 +281,10 @@ def tile_wavernncell_pa_t_kernel(tc, x, feat, aux1, h, w_ih, w_hh, b_ih, b_hh, o
                     }
                 pw = pairs[w]
                 a1 = ew.tile([P, BB], F32, tag="a1", name="a1")
-                a2 = ew.tile([P, BB], F32, tag="a2", name="a2")
-                x_terms(i, 0, gi_r, gh_r, a1[:], a2[:])
-                nc.vector.tensor_tensor(out=a1[:], in0=a1[:], in1=a2[:], op=ALU.add)
+                xbv = loaded[blk][2][:].rearrange("p (b i) -> p b i", i=2)
+                nc.vector.scalar_tensor_tensor(out=a1[:], in0=xbv[:, :, 0], scalar=wx[:, 0, u, e, 0:1], in1=gi_r[:], op0=ALU.mult, op1=ALU.add)
+                nc.vector.scalar_tensor_tensor(out=a1[:], in0=staged[blk][4][:], scalar=wx[:, 0, u, e, 1:2], in1=a1[:], op0=ALU.mult, op1=ALU.add)
+                nc.vector.tensor_tensor(out=a1[:], in0=gh_r[:], in1=a1[:], op=ALU.add)
                 r = ew.tile([P, BB], F32, tag="r", name="r")
                 nc.scalar.activation(out=r[:], in_=a1[:], func=ACT.Sigmoid, bias=brz[:, c:c + 1], scale=1.0)
             if i % 2 == 0 and 2 <= i <= NUNIT:
@@ -307,6 +317,8 @@ def tile_wavernncell_pa_t_kernel(tc, x, feat, aux1, h, w_ih, w_hh, b_ih, b_hh, o
                 nc.scalar.activation(out=pw["n"][:, e, :], in_=v[:], func=ACT.Tanh, bias=bias[:, 8 + c:9 + c], scale=1.0)
                 if c == 2 and nxt < NBLK:
                     stage_q(nxt)
+                if c == 3 and nxt < NBLK:
+                    x1_bank(nxt)
                 if e == 1:
                     pw["d"] = ew.tile([P, 2, BB], F32, tag="d", name="d", bufs=3)
                     ht = staged[blk][0][:].rearrange("p (b t) -> p t b", t=4)[:, 2 * u:2 * u + 2, :]

@@ -192,38 +192,38 @@ def tile_wavernncell_pa_t_kernel(tc, x, feat, aux1, h, w_ih, w_hh, b_ih, b_hh, o
         x1_bank(0)
 
         pairs = {}
+        units = {}
 
-        def matmuls(i):
+        def mm_mx(i, g):
             blk, c = divmod(i, 4)
-            hc, hs, catt = staged[blk][1], staged[blk][2], staged[blk][3]
-            cb = catt[:].bitcast(BF16).rearrange("p (b e) -> p b e", e=2)
-            res = []
-            for g in range(3):
-                q = g * 4 + c
-                gh = psum.tile([P, BB], F32, tag="gh", name="gh")
-                nc.tensor.matmul_mx(
-                    out=gh[:],
-                    lhsT=wc[:, q * P:(q + 1) * P].bitcast(FP8X4),
-                    lhsT_scale=wsc[:, q * P:(q + 1) * P],
-                    rhs=hc[:].bitcast(FP8X4),
-                    rhs_scale=hs[:],
-                    start=True,
-                    stop=True,
-                )
-                gi = psum.tile([P, BB], F32, tag="gi", name="gi", bufs=2)
-                nc.tensor.matmul(gi[:], lhsT=wiht[:, 0, q, :], rhs=cb[:, :, 0], start=True, stop=False)
-                nc.tensor.matmul(gi[:], lhsT=wiht[:, 1, q, :], rhs=cb[:, :, 1], start=False, stop=(g < 2))
-                if g == 2:
-                    nc.tensor.matmul(gi[:], lhsT=xw[:, c, :], rhs=xmv[:, blk * BB:(blk + 1) * BB, 0], start=False, stop=True)
-                res.append((gi, gh))
-            return res
+            q = g * 4 + c
+            gh = psum.tile([P, BB], F32, tag="gh", name="gh")
+            nc.tensor.matmul_mx(
+                out=gh[:],
+                lhsT=wc[:, q * P:(q + 1) * P].bitcast(FP8X4),
+                lhsT_scale=wsc[:, q * P:(q + 1) * P],
+                rhs=staged[blk][1][:].bitcast(FP8X4),
+                rhs_scale=staged[blk][2][:],
+                start=True,
+                stop=True,
+            )
+            return gh
 
-        def x_terms(i, g, gi, gh, o1, o2):
+        def mm_plain(i, g):
             blk, c = divmod(i, 4)
-            u, e = divmod(c, 2)
+            q = g * 4 + c
+            cb = staged[blk][3][:].bitcast(BF16).rearrange("p (b e) -> p b e", e=2)
+            gi = psum.tile([P, BB], F32, tag="gi", name="gi", bufs=2)
+            nc.tensor.matmul(gi[:], lhsT=wiht[:, 0, q, :], rhs=cb[:, :, 0], start=True, stop=False)
+            nc.tensor.matmul(gi[:], lhsT=wiht[:, 1, q, :], rhs=cb[:, :, 1], start=False, stop=(g < 2))
+            if g == 2:
+                nc.tensor.matmul(gi[:], lhsT=xw[:, c, :], rhs=xmv[:, blk * BB:(blk + 1) * BB, 0], start=False, stop=True)
+            return gi
+
+        def x_term(i, g, t, dst, acc):
+            blk, c = divmod(i, 4)
             xbv = loaded[blk][2][:].rearrange("p (b i) -> p b i", i=2)
-            nc.vector.scalar_tensor_tensor(out=o2, in0=xbv[:, :, 1], scalar=wx[:, g, u, e, 1:2], in1=gh[:], op0=ALU.mult, op1=ALU.add)
-            nc.vector.scalar_tensor_tensor(out=o1, in0=xbv[:, :, 0], scalar=wx[:, g, u, e, 0:1], in1=gi[:], op0=ALU.mult, op1=ALU.add)
+            nc.vector.scalar_tensor_tensor(out=dst, in0=xbv[:, :, t], scalar=wx[:, g, c // 2, c % 2, t:t + 1], in1=acc, op0=ALU.mult, op1=ALU.add)
 
         def out_t(k, ps):
             w, sp = divmod(k, 2)
@@ -231,11 +231,8 @@ def tile_wavernncell_pa_t_kernel(tc, x, feat, aux1, h, w_ih, w_hh, b_ih, b_hh, o
             for s2 in range(2):
                 for e in range(2):
                     lo = (2 * sp + s2) * P
-                    if ACC:
-                        nc.tensor.matmul(ps[:, s2, e, :], lhsT=dd[:, e, lo:lo + P], rhs=ident_f[:], is_transpose=True, start=True, stop=False)
-                        nc.tensor.matmul(ps[:, s2, e, :], lhsT=nn[:, e, lo:lo + P], rhs=ident_f[:], is_transpose=True, start=False, stop=True)
-                    else:
-                        nc.tensor.transpose(ps[:, s2, e, :], dd[:, e, lo:lo + P], ident_f[:])
+                    nc.tensor.matmul(ps[:, s2, e, :], lhsT=dd[:, e, lo:lo + P], rhs=ident_f[:], is_transpose=True, start=True, stop=False)
+                    nc.tensor.matmul(ps[:, s2, e, :], lhsT=nn[:, e, lo:lo + P], rhs=ident_f[:], is_transpose=True, start=False, stop=True)
 
         def out_c(k, ps, on_vector):
             w, sp = divmod(k, 2)
@@ -250,17 +247,30 @@ def tile_wavernncell_pa_t_kernel(tc, x, feat, aux1, h, w_ih, w_hh, b_ih, b_hh, o
             r0 = blk * BB + sp * 256
             nc.sync.dma_start(out=out[r0:r0 + 256, u * 256:(u + 1) * 256].rearrange("(s b) j -> b s j", b=P), in_=ob[:])
 
-        for i in range(NUNIT + OUT_LAG):
-            blk, c = divmod(i, 4)
+        for j in range(NUNIT + OUT_LAG):
+            blk, c = divmod(j, 4)
             u, e = divmod(c, 2)
-            w = i // 2
-            live = i < NUNIT
+            w = j // 2
+            live = j < NUNIT
+            lag = 1 <= j <= NUNIT
+            jn = j - 1
+            cn = jn % 4
+            wn = jn // 2
             nxt = blk + 1
-            k = i - OUT_LAG
+            k = j - OUT_LAG
             if live:
                 if c == 0 and blk + 2 < NBLK:
                     load(blk + 2)
-                (gi_r, gh_r), (gi_z, gh_z), (gi_n, gh_n) = matmuls(i)
+                gi_r = mm_plain(j, 0)
+            if lag:
+                gh_n = mm_mx(jn, 2)
+            if live:
+                gi_z = mm_plain(j, 1)
+                gh_r = mm_mx(j, 0)
+            if lag:
+                gi_n = mm_plain(jn, 2)
+            if live:
+                gh_z = mm_mx(j, 1)
             ps_o = None
             if 0 <= k:
                 ps_o = psum.tile([P, 2, 2, P], F32, tag="tp", name="ps_o", bufs=2)
@@ -281,13 +291,32 @@ def tile_wavernncell_pa_t_kernel(tc, x, feat, aux1, h, w_ih, w_hh, b_ih, b_hh, o
                     }
                 pw = pairs[w]
                 a1 = ew.tile([P, BB], F32, tag="a1", name="a1")
-                xbv = loaded[blk][2][:].rearrange("p (b i) -> p b i", i=2)
-                nc.vector.scalar_tensor_tensor(out=a1[:], in0=xbv[:, :, 0], scalar=wx[:, 0, u, e, 0:1], in1=gi_r[:], op0=ALU.mult, op1=ALU.add)
+                x_term(j, 0, 0, a1[:], gi_r[:])
+            if lag:
+                v = ew.tile([P, BB], F32, tag="v", name="v")
+                nc.vector.scalar_tensor_tensor(out=v[:], in0=gh_n[:], scalar=bias[:, 20 + cn:21 + cn], in1=units[jn][:], op0=ALU.add, op1=ALU.mult)
+            if live:
                 nc.vector.scalar_tensor_tensor(out=a1[:], in0=staged[blk][4][:], scalar=wx[:, 0, u, e, 1:2], in1=a1[:], op0=ALU.mult, op1=ALU.add)
+                x_term(j, 1, 0, pw["a1"][:, e, :], gi_z[:])
                 nc.vector.tensor_tensor(out=a1[:], in0=gh_r[:], in1=a1[:], op=ALU.add)
                 r = ew.tile([P, BB], F32, tag="r", name="r")
                 nc.scalar.activation(out=r[:], in_=a1[:], func=ACT.Sigmoid, bias=brz[:, c:c + 1], scale=1.0)
-            if i % 2 == 0 and 2 <= i <= NUNIT:
+                units[j] = r
+            if lag:
+                pn = pairs[wn]
+                nc.vector.tensor_tensor(out=v[:], in0=gi_n[:], in1=v[:], op=ALU.add)
+                nc.scalar.activation(out=pn["n"][:, cn % 2, :], in_=v[:], func=ACT.Tanh, bias=bias[:, 8 + cn:9 + cn], scale=1.0)
+                if cn % 2 == 1:
+                    pn["d"] = ew.tile([P, 2, BB], F32, tag="d", name="d", bufs=3)
+                    un = cn // 2
+                    ht = staged[jn // 4][0][:].rearrange("p (b t) -> p t b", t=4)[:, 2 * un:2 * un + 2, :]
+                    eng = nc.vector if wn == NPAIR - 1 else nc.gpsimd
+                    eng.tensor_tensor(out=pn["d"][:], in0=ht, in1=pn["n"][:], op=ALU.subtract)
+            if live:
+                x_term(j, 1, 1, pw["a2"][:, e, :], gh_z[:])
+                if e == 1:
+                    nc.gpsimd.tensor_tensor(out=pw["a1"][:], in0=pw["a1"][:], in1=pw["a2"][:], op=ALU.add)
+            if j % 2 == 0 and 2 <= j <= NUNIT:
                 wp = w - 1
                 pp = pairs[wp]
                 up = wp % 2
@@ -297,12 +326,6 @@ def tile_wavernncell_pa_t_kernel(tc, x, feat, aux1, h, w_ih, w_hh, b_ih, b_hh, o
                     nc.scalar.activation(out=z[:, ez, :], in_=pp["a1"][:, ez, :], func=ACT.Sigmoid, bias=brz[:, cz:cz + 1], scale=1.0)
                 eng = nc.vector if wp == NPAIR - 1 else nc.gpsimd
                 eng.tensor_tensor(out=pp["d"][:], in0=pp["d"][:], in1=z[:], op=ALU.mult)
-                if not ACC:
-                    eng.tensor_tensor(out=pp["d"][:], in0=pp["d"][:], in1=pp["n"][:], op=ALU.add)
-            if live:
-                x_terms(i, 1, gi_z, gh_z, pw["a1"][:, e, :], pw["a2"][:, e, :])
-                if e == 1:
-                    nc.gpsimd.tensor_tensor(out=pw["a1"][:], in0=pw["a1"][:], in1=pw["a2"][:], op=ALU.add)
             if ps_i is not None:
                 if c < 2:
                     stage_h_c(nxt, c, ps_i)
@@ -311,16 +334,7 @@ def tile_wavernncell_pa_t_kernel(tc, x, feat, aux1, h, w_ih, w_hh, b_ih, b_hh, o
             if ps_o is not None:
                 out_c(k, ps_o, (not live) and k % 2 == 1)
             if live:
-                v = ew.tile([P, BB], F32, tag="v", name="v")
-                nc.vector.scalar_tensor_tensor(out=v[:], in0=gh_n[:], scalar=bias[:, 20 + c:21 + c], in1=r[:], op0=ALU.add, op1=ALU.mult)
-                nc.vector.tensor_tensor(out=v[:], in0=gi_n[:], in1=v[:], op=ALU.add)
-                nc.scalar.activation(out=pw["n"][:, e, :], in_=v[:], func=ACT.Tanh, bias=bias[:, 8 + c:9 + c], scale=1.0)
                 if c == 2 and nxt < NBLK:
                     stage_q(nxt)
                 if c == 3 and nxt < NBLK:
                     x1_bank(nxt)
-                if e == 1:
-                    pw["d"] = ew.tile([P, 2, BB], F32, tag="d", name="d", bufs=3)
-                    ht = staged[blk][0][:].rearrange("p (b t) -> p t b", t=4)[:, 2 * u:2 * u + 2, :]
-                    eng = nc.vector if w == NPAIR - 1 else nc.gpsimd
-                    eng.tensor_tensor(out=pw["d"][:], in0=ht, in1=pw["n"][:], op=ALU.subtract)

@@ -54,7 +54,7 @@ def tile_wavernncell_pa_t_kernel(tc, x, feat, aux1, h, w_ih, w_hh, b_ih, b_hh, o
         t4 = const.tile([P, 4, P], BF16, name="t4")
         nc.vector.memset(t4[:], 0.0)
         xm = const.tile([P, 2 * B], BF16, name="xm")
-        nc.vector.memset(xm[:], 0.0)
+        nc.vector.memset(xm[:].bitcast(mybir.dt.int32), 0)
 
         whh_sb = const.tile([P, 3, 2, 1024], BF16, name="whh_sb")
         wih_sb = const.tile([P, 3, 2, WROW], BF16, name="wih_sb")
@@ -86,6 +86,8 @@ def tile_wavernncell_pa_t_kernel(tc, x, feat, aux1, h, w_ih, w_hh, b_ih, b_hh, o
         def load(blk):
             h_sb = ld.tile([P, 4, H], BF16, tag="h", name="h_sb")
             nc.sync.dma_start(out=h_sb[:], in_=h[blk * BB:(blk + 1) * BB, :].rearrange("(s p) k -> p s k", p=P))
+            if blk == 0:
+                nc.sync.dma_start(out=wih_sb[:, :, 0, 0:516], in_=wih_v[:, :, 0, :])
             cat = ld.tile([P, 4, 256], BF16, tag="cat", name="cat")
             nc.sync.dma_start(out=cat[:, :, 0:128], in_=feat[blk * BB:(blk + 1) * BB, :].rearrange("(s p) k -> p s k", p=P))
             nc.sync.dma_start(out=cat[:, :, 128:256], in_=aux1[blk * BB:(blk + 1) * BB, :].rearrange("(s p) k -> p s k", p=P))
@@ -136,60 +138,83 @@ def tile_wavernncell_pa_t_kernel(tc, x, feat, aux1, h, w_ih, w_hh, b_ih, b_hh, o
                 in_=wgrp[:, gu * 1024:(gu + 1) * 1024],
             )
 
-        def prep_w(u):
-            for g in range(3):
-                gu = g * 2 + u
-                ps = any_bank([P, 2, 2, P], F32)
-                for e in range(2):
-                    for uu in range(2):
-                        lo = e * 256 + uu * P
-                        nc.tensor.transpose(ps[:, uu, e, :], whh_w[:, g, u, lo:lo + P], ident_f[:])
-                dst = wgrp_w[:, gu * 512:(gu + 1) * 512].rearrange("p (e m k) -> p e m k", e=2, k=2)
-                nc.vector.tensor_copy(out=dst, in_=ps[:].rearrange("p k e m -> p e m k"))
-                if g > 0:
-                    quant_w(gu - 2)
-            for g in range(3):
-                gu = g * 2 + u
-                ps2 = any_bank([P, 2, P], F32)
-                for e in range(2):
-                    nc.tensor.transpose(ps2[:, e, :], wih_w[:, g, u, e * 129:e * 129 + P], ident_f[:])
-                src = ps2[:].bitcast(BF16).rearrange("w e (m k) -> w k e m", k=2)
-                nc.scalar.copy(out=wiht[:, :, gu * 2:gu * 2 + 2, :], in_=src)
-            quant_w(4 + u)
+        def whh_t(g, u, ps):
+            for e in range(2):
+                for uu in range(2):
+                    lo = e * 256 + uu * P
+                    nc.tensor.transpose(ps[:, uu, e, :], whh_w[:, g, u, lo:lo + P], ident_f[:])
+
+        def whh_c(g, u, ps, on_vector):
+            gu = g * 2 + u
+            dst = wgrp_w[:, gu * 512:(gu + 1) * 512].rearrange("p (e m k) -> p e m k", e=2, k=2)
+            src = ps[:].rearrange("p k e m -> p e m k")
+            if on_vector:
+                nc.vector.tensor_copy(out=dst, in_=src)
+            else:
+                nc.scalar.copy(out=dst, in_=src)
+
+        def wih_t(g, u, ps, slot):
+            for e in range(2):
+                nc.tensor.transpose(ps[:, slot, e, :], wih_w[:, g, u, e * 129:e * 129 + P], ident_f[:])
+
+        def wih_c(g, u, ps, slot):
+            gu = g * 2 + u
+            src = ps[:, slot, :, :].bitcast(BF16).rearrange("w e (m k) -> w k e m", k=2)
+            nc.scalar.copy(out=wiht[:, :, gu * 2:gu * 2 + 2, :], in_=src)
+
+        def wx_c(u):
             nc.vector.tensor_copy(out=wx[:, :, u, :, :], in_=wih5[:, :, u, :, 256:258])
             nc.vector.tensor_copy(out=t4[:, u * 2:u * 2 + 2, 0:2], in_=wih5[:, 2, u, :, 256:258])
 
-        nc.sync.dma_start(out=whh_sb[:, :, 0, :], in_=whh_v[:, :, 0, :])
-        nc.sync.dma_start(out=wih_sb[:, :, 0, 0:516], in_=wih_v[:, :, 0, :])
-        nc.sync.dma_start(out=whh_sb[:, :, 1, :], in_=whh_v[:, :, 1, :])
-        nc.sync.dma_start(out=wih_sb[:, :, 1, 0:516], in_=wih_v[:, :, 1, :])
-        load(0)
-        nc.sync.dma_start(out=xs[:], in_=x.rearrange("(t p) i -> p t i", p=P))
+        def xw_t(u, ps):
+            for e in range(2):
+                nc.tensor.transpose(ps[:, e, :], t4[:, u * 2 + e, :], ident_b[:])
+
+        def xw_c(u, ps):
+            nc.vector.tensor_copy(out=xw[:, u * 2:u * 2 + 2, :], in_=ps[:])
+
+        xs_v = x.rearrange("(t p) i -> p t i", p=P)
+        nc.sync.dma_start(out=xs[:, 0:8, :], in_=xs_v[:, 0:8, :])
         nc.sync.dma_start(out=brow[0:6, :], in_=b_ih.rearrange("(r c) -> r c", c=256))
         nc.sync.dma_start(out=brow[6:12, :], in_=b_hh.rearrange("(r c) -> r c", c=256))
+        for g in range(3):
+            nc.sync.dma_start(out=whh_sb[:, g, 0, :], in_=whh_v[:, g, 0, :])
+        load(0)
         nc.sync.dma_start(out=xm[0:1, :], in_=xf.unsqueeze(0))
         nc.sync.dma_start(out=xm[1:2, 0:2 * B - 1], in_=xf[1:2 * B].unsqueeze(0))
+        nc.sync.dma_start(out=wih_sb[:, :, 1, 0:516], in_=wih_v[:, :, 1, :])
+        nc.sync.dma_start(out=whh_sb[:, :, 1, :], in_=whh_v[:, :, 1, :])
         load(1)
+        nc.sync.dma_start(out=xs[:, 8:B // P, :], in_=xs_v[:, 8:B // P, :])
 
-        prep_w(0)
-        prep_w(1)
-        psx = any_bank([P, 4, P], BF16)
-        for c in range(4):
-            nc.tensor.transpose(psx[:, c, :], t4[:, c, :], ident_b[:])
-        nc.vector.tensor_copy(out=xw[:], in_=psx[:])
-        for half in range(2):
-            ps = any_bank([P, 2, 2, P], F32)
-            stage_h_t(0, half, ps)
-            stage_h_c(0, half, ps)
-        ps = any_bank([P, 2, 2, P], F32)
-        stage_cat_t(0, ps)
-        stage_cat_c(0, ps)
         psb = any_bank([P, P], F32)
         nc.tensor.transpose(psb[:], brow[:].bitcast(F32), ident_f[:])
         nc.vector.tensor_copy(out=bias[:], in_=psb[:].bitcast(BF16)[:, 0:24])
         nc.vector.tensor_tensor(out=brz[:], in0=bias[:, 0:8], in1=bias[:, 12:20], op=ALU.add)
-        stage_q(0)
+        for g in range(3):
+            ps = any_bank([P, 2, 2, P], F32)
+            whh_t(g, 0, ps)
+            whh_c(g, 0, ps, True)
+            if g > 0:
+                quant_w(2 * g - 2)
+        quant_w(4)
+        for half in range(2):
+            ps = any_bank([P, 2, 2, P], F32)
+            stage_h_t(0, half, ps)
+            stage_h_c(0, half, ps)
         x1_bank(0)
+        for g in range(3):
+            ps = any_bank([P, 2, 2, P], F32)
+            wih_t(g, 0, ps, 0)
+            wih_c(g, 0, ps, 0)
+        stage_q(0)
+        wx_c(0)
+        psx = any_bank([P, 2, P], BF16)
+        xw_t(0, psx)
+        xw_c(0, psx)
+        ps = any_bank([P, 2, 2, P], F32)
+        stage_cat_t(0, ps)
+        stage_cat_c(0, ps)
 
         pairs = {}
         units = {}
@@ -219,6 +244,9 @@ def tile_wavernncell_pa_t_kernel(tc, x, feat, aux1, h, w_ih, w_hh, b_ih, b_hh, o
             if g == 2:
                 nc.tensor.matmul(gi[:], lhsT=xw[:, c, :], rhs=xmv[:, blk * BB:(blk + 1) * BB, 0], start=False, stop=True)
             return gi
+
+        def e_bank():
+            return psum.tile([P, 2, 2, P], F32, tag="tp", name="ps_e", bufs=2)
 
         def x_term(i, g, t, dst, acc):
             blk, c = divmod(i, 4)
@@ -264,13 +292,23 @@ def tile_wavernncell_pa_t_kernel(tc, x, feat, aux1, h, w_ih, w_hh, b_ih, b_hh, o
                 gi_r = mm_plain(j, 0)
             if lag:
                 gh_n = mm_mx(jn, 2)
+            eb = {}
+            if j == 1:
+                eb["h0"] = e_bank()
+                whh_t(0, 1, eb["h0"])
             if live:
                 gi_z = mm_plain(j, 1)
                 gh_r = mm_mx(j, 0)
-            if lag:
-                gi_n = mm_plain(jn, 2)
+            if j == 1:
+                eb["h1"] = e_bank()
+                whh_t(1, 1, eb["h1"])
             if live:
                 gh_z = mm_mx(j, 1)
+            if lag:
+                gi_n = mm_plain(jn, 2)
+            if j == 1:
+                eb["h2"] = e_bank()
+                whh_t(2, 1, eb["h2"])
             ps_o = None
             if 0 <= k:
                 ps_o = psum.tile([P, 2, 2, P], F32, tag="tp", name="ps_o", bufs=2)
@@ -282,13 +320,29 @@ def tile_wavernncell_pa_t_kernel(tc, x, feat, aux1, h, w_ih, w_hh, b_ih, b_hh, o
                     stage_h_t(nxt, c, ps_i)
                 else:
                     stage_cat_t(nxt, ps_i)
+            if j == 0:
+                eb["ia"] = e_bank()
+                wih_t(0, 1, eb["ia"], 0)
+                wih_t(1, 1, eb["ia"], 1)
+                eb["ib"] = e_bank()
+                wih_t(2, 1, eb["ib"], 0)
+                stage_h_c(nxt, c, ps_i)
+                wih_c(0, 1, eb["ia"], 0)
+                wih_c(1, 1, eb["ia"], 1)
+            if j == 1:
+                whh_c(0, 1, eb["h0"], False)
+                whh_c(1, 1, eb["h1"], False)
+            if j == 2:
+                psx = psum.tile([P, 2, P], BF16, tag="tp", name="ps_x", bufs=2)
+                xw_t(1, psx)
             if live:
                 if e == 0:
                     pairs[w] = {
                         "a1": ew.tile([P, 2, BB], F32, tag="az1", name="az1"),
-                        "a2": ew.tile([P, 2, BB], F32, tag="az2", name="az2"),
                         "n": ew.tile([P, 2, BB], F32, tag="n", name="n", bufs=3),
                     }
+                    if w < NPAIR - 1:
+                        pairs[w]["a2"] = ew.tile([P, 2, BB], F32, tag="az2", name="az2")
                 pw = pairs[w]
                 a1 = ew.tile([P, BB], F32, tag="a1", name="a1")
                 x_term(j, 0, 0, a1[:], gi_r[:])
@@ -302,21 +356,39 @@ def tile_wavernncell_pa_t_kernel(tc, x, feat, aux1, h, w_ih, w_hh, b_ih, b_hh, o
                 r = ew.tile([P, BB], F32, tag="r", name="r")
                 nc.scalar.activation(out=r[:], in_=a1[:], func=ACT.Sigmoid, bias=brz[:, c:c + 1], scale=1.0)
                 units[j] = r
+                if j == 0:
+                    wih_c(2, 1, eb["ib"], 0)
             if lag:
                 pn = pairs[wn]
                 nc.vector.tensor_tensor(out=v[:], in0=gi_n[:], in1=v[:], op=ALU.add)
                 nc.scalar.activation(out=pn["n"][:, cn % 2, :], in_=v[:], func=ACT.Tanh, bias=bias[:, 8 + cn:9 + cn], scale=1.0)
-                if cn % 2 == 1:
+                if j == 1:
+                    whh_c(2, 1, eb["h2"], False)
+                if wn == NPAIR - 1:
+                    en = cn % 2
+                    if en == 0:
+                        pn["d"] = ew.tile([P, 2, BB], F32, tag="d", name="d", bufs=3)
+                    ht = staged[jn // 4][0][:].rearrange("p (b t) -> p b t", t=4)[:, :, cn]
+                    eng = nc.gpsimd if en == 0 else nc.vector
+                    eng.tensor_tensor(out=pn["d"][:, en, :], in0=ht, in1=pn["n"][:, en, :], op=ALU.subtract)
+                    eng.tensor_tensor(out=pn["d"][:, en, :], in0=pn["d"][:, en, :], in1=pn["z"][:, en, :], op=ALU.mult)
+                elif cn % 2 == 1:
                     pn["d"] = ew.tile([P, 2, BB], F32, tag="d", name="d", bufs=3)
                     un = cn // 2
                     ht = staged[jn // 4][0][:].rearrange("p (b t) -> p t b", t=4)[:, 2 * un:2 * un + 2, :]
-                    eng = nc.vector if wn == NPAIR - 1 else nc.gpsimd
-                    eng.tensor_tensor(out=pn["d"][:], in0=ht, in1=pn["n"][:], op=ALU.subtract)
-            if live:
+                    nc.gpsimd.tensor_tensor(out=pn["d"][:], in0=ht, in1=pn["n"][:], op=ALU.subtract)
+            if live and w == NPAIR - 1:
+                if e == 0:
+                    pw["z"] = ew.tile([P, 2, BB], F32, tag="z", name="z")
+                az = pw["a1"][:, e, :]
+                nc.vector.scalar_tensor_tensor(out=az, in0=staged[blk][4][:], scalar=wx[:, 1, u, e, 1:2], in1=az, op0=ALU.mult, op1=ALU.add)
+                nc.vector.tensor_tensor(out=az, in0=gh_z[:], in1=az, op=ALU.add)
+                nc.scalar.activation(out=pw["z"][:, e, :], in_=az, func=ACT.Sigmoid, bias=brz[:, 4 + c:5 + c], scale=1.0)
+            elif live:
                 x_term(j, 1, 1, pw["a2"][:, e, :], gh_z[:])
                 if e == 1:
                     nc.gpsimd.tensor_tensor(out=pw["a1"][:], in0=pw["a1"][:], in1=pw["a2"][:], op=ALU.add)
-            if j % 2 == 0 and 2 <= j <= NUNIT:
+            if j % 2 == 0 and 2 <= j < NUNIT:
                 wp = w - 1
                 pp = pairs[wp]
                 up = wp % 2
@@ -324,15 +396,22 @@ def tile_wavernncell_pa_t_kernel(tc, x, feat, aux1, h, w_ih, w_hh, b_ih, b_hh, o
                 for ez in range(2):
                     cz = 4 + 2 * up + ez
                     nc.scalar.activation(out=z[:, ez, :], in_=pp["a1"][:, ez, :], func=ACT.Sigmoid, bias=brz[:, cz:cz + 1], scale=1.0)
-                eng = nc.vector if wp == NPAIR - 1 else nc.gpsimd
-                eng.tensor_tensor(out=pp["d"][:], in0=pp["d"][:], in1=z[:], op=ALU.mult)
-            if ps_i is not None:
+                nc.gpsimd.tensor_tensor(out=pp["d"][:], in0=pp["d"][:], in1=z[:], op=ALU.mult)
+            if ps_i is not None and j > 0:
                 if c < 2:
                     stage_h_c(nxt, c, ps_i)
                 else:
                     stage_cat_c(nxt, ps_i)
             if ps_o is not None:
                 out_c(k, ps_o, (not live) and k % 2 == 1)
+            if j == 0:
+                wx_c(1)
+            if j == 1:
+                quant_w(1)
+                quant_w(3)
+            if j == 2:
+                quant_w(5)
+                xw_c(1, psx)
             if live:
                 if c == 2 and nxt < NBLK:
                     stage_q(nxt)

@@ -54,7 +54,7 @@ def tile_wavernncell_pa_t_kernel(tc, x, feat, aux1, h, w_ih, w_hh, b_ih, b_hh, o
         t4 = const.tile([P, 4, P], BF16, name="t4")
         nc.vector.memset(t4[:], 0.0)
         xm = const.tile([P, 2 * B], BF16, name="xm")
-        nc.vector.memset(xm[:].bitcast(mybir.dt.int32), 0)
+        nc.vector.memset(xm[:], 0.0)
 
         whh_sb = const.tile([P, 3, 2, 1024], BF16, name="whh_sb")
         wih_sb = const.tile([P, 3, 2, WROW], BF16, name="wih_sb")
@@ -86,8 +86,6 @@ def tile_wavernncell_pa_t_kernel(tc, x, feat, aux1, h, w_ih, w_hh, b_ih, b_hh, o
         def load(blk):
             h_sb = ld.tile([P, 4, H], BF16, tag="h", name="h_sb")
             nc.sync.dma_start(out=h_sb[:], in_=h[blk * BB:(blk + 1) * BB, :].rearrange("(s p) k -> p s k", p=P))
-            if blk == 0:
-                nc.sync.dma_start(out=wih_sb[:, :, 0, 0:516], in_=wih_v[:, :, 0, :])
             cat = ld.tile([P, 4, 256], BF16, tag="cat", name="cat")
             nc.sync.dma_start(out=cat[:, :, 0:128], in_=feat[blk * BB:(blk + 1) * BB, :].rearrange("(s p) k -> p s k", p=P))
             nc.sync.dma_start(out=cat[:, :, 128:256], in_=aux1[blk * BB:(blk + 1) * BB, :].rearrange("(s p) k -> p s k", p=P))
@@ -138,83 +136,60 @@ def tile_wavernncell_pa_t_kernel(tc, x, feat, aux1, h, w_ih, w_hh, b_ih, b_hh, o
                 in_=wgrp[:, gu * 1024:(gu + 1) * 1024],
             )
 
-        def whh_t(g, u, ps):
-            for e in range(2):
-                for uu in range(2):
-                    lo = e * 256 + uu * P
-                    nc.tensor.transpose(ps[:, uu, e, :], whh_w[:, g, u, lo:lo + P], ident_f[:])
-
-        def whh_c(g, u, ps, on_vector):
-            gu = g * 2 + u
-            dst = wgrp_w[:, gu * 512:(gu + 1) * 512].rearrange("p (e m k) -> p e m k", e=2, k=2)
-            src = ps[:].rearrange("p k e m -> p e m k")
-            if on_vector:
-                nc.vector.tensor_copy(out=dst, in_=src)
-            else:
-                nc.scalar.copy(out=dst, in_=src)
-
-        def wih_t(g, u, ps, slot):
-            for e in range(2):
-                nc.tensor.transpose(ps[:, slot, e, :], wih_w[:, g, u, e * 129:e * 129 + P], ident_f[:])
-
-        def wih_c(g, u, ps, slot):
-            gu = g * 2 + u
-            src = ps[:, slot, :, :].bitcast(BF16).rearrange("w e (m k) -> w k e m", k=2)
-            nc.scalar.copy(out=wiht[:, :, gu * 2:gu * 2 + 2, :], in_=src)
-
-        def wx_c(u):
+        def prep_w(u):
+            for g in range(3):
+                gu = g * 2 + u
+                ps = any_bank([P, 2, 2, P], F32)
+                for e in range(2):
+                    for uu in range(2):
+                        lo = e * 256 + uu * P
+                        nc.tensor.transpose(ps[:, uu, e, :], whh_w[:, g, u, lo:lo + P], ident_f[:])
+                dst = wgrp_w[:, gu * 512:(gu + 1) * 512].rearrange("p (e m k) -> p e m k", e=2, k=2)
+                nc.vector.tensor_copy(out=dst, in_=ps[:].rearrange("p k e m -> p e m k"))
+                if g > 0:
+                    quant_w(gu - 2)
+            for g in range(3):
+                gu = g * 2 + u
+                ps2 = any_bank([P, 2, P], F32)
+                for e in range(2):
+                    nc.tensor.transpose(ps2[:, e, :], wih_w[:, g, u, e * 129:e * 129 + P], ident_f[:])
+                src = ps2[:].bitcast(BF16).rearrange("w e (m k) -> w k e m", k=2)
+                nc.scalar.copy(out=wiht[:, :, gu * 2:gu * 2 + 2, :], in_=src)
+            quant_w(4 + u)
             nc.vector.tensor_copy(out=wx[:, :, u, :, :], in_=wih5[:, :, u, :, 256:258])
             nc.vector.tensor_copy(out=t4[:, u * 2:u * 2 + 2, 0:2], in_=wih5[:, 2, u, :, 256:258])
 
-        def xw_t(u, ps):
-            for e in range(2):
-                nc.tensor.transpose(ps[:, e, :], t4[:, u * 2 + e, :], ident_b[:])
-
-        def xw_c(u, ps):
-            nc.vector.tensor_copy(out=xw[:, u * 2:u * 2 + 2, :], in_=ps[:])
-
-        xs_v = x.rearrange("(t p) i -> p t i", p=P)
-        nc.sync.dma_start(out=xs[:, 0:8, :], in_=xs_v[:, 0:8, :])
+        nc.sync.dma_start(out=whh_sb[:, :, 0, :], in_=whh_v[:, :, 0, :])
+        nc.sync.dma_start(out=wih_sb[:, :, 0, 0:516], in_=wih_v[:, :, 0, :])
+        nc.sync.dma_start(out=whh_sb[:, :, 1, :], in_=whh_v[:, :, 1, :])
+        nc.sync.dma_start(out=wih_sb[:, :, 1, 0:516], in_=wih_v[:, :, 1, :])
+        load(0)
+        nc.sync.dma_start(out=xs[:], in_=x.rearrange("(t p) i -> p t i", p=P))
         nc.sync.dma_start(out=brow[0:6, :], in_=b_ih.rearrange("(r c) -> r c", c=256))
         nc.sync.dma_start(out=brow[6:12, :], in_=b_hh.rearrange("(r c) -> r c", c=256))
-        for g in range(3):
-            nc.sync.dma_start(out=whh_sb[:, g, 0, :], in_=whh_v[:, g, 0, :])
-        load(0)
         nc.sync.dma_start(out=xm[0:1, :], in_=xf.unsqueeze(0))
         nc.sync.dma_start(out=xm[1:2, 0:2 * B - 1], in_=xf[1:2 * B].unsqueeze(0))
-        nc.sync.dma_start(out=wih_sb[:, :, 1, 0:516], in_=wih_v[:, :, 1, :])
-        nc.sync.dma_start(out=whh_sb[:, :, 1, :], in_=whh_v[:, :, 1, :])
         load(1)
-        nc.sync.dma_start(out=xs[:, 8:B // P, :], in_=xs_v[:, 8:B // P, :])
 
-        psb = any_bank([P, P], F32)
-        nc.tensor.transpose(psb[:], brow[:].bitcast(F32), ident_f[:])
-        nc.vector.tensor_copy(out=bias[:], in_=psb[:].bitcast(BF16)[:, 0:24])
-        nc.vector.tensor_tensor(out=brz[:], in0=bias[:, 0:8], in1=bias[:, 12:20], op=ALU.add)
-        for g in range(3):
-            ps = any_bank([P, 2, 2, P], F32)
-            whh_t(g, 0, ps)
-            whh_c(g, 0, ps, True)
-            if g > 0:
-                quant_w(2 * g - 2)
-        quant_w(4)
+        prep_w(0)
+        prep_w(1)
+        psx = any_bank([P, 4, P], BF16)
+        for c in range(4):
+            nc.tensor.transpose(psx[:, c, :], t4[:, c, :], ident_b[:])
+        nc.vector.tensor_copy(out=xw[:], in_=psx[:])
         for half in range(2):
             ps = any_bank([P, 2, 2, P], F32)
             stage_h_t(0, half, ps)
             stage_h_c(0, half, ps)
-        x1_bank(0)
-        for g in range(3):
-            ps = any_bank([P, 2, 2, P], F32)
-            wih_t(g, 0, ps, 0)
-            wih_c(g, 0, ps, 0)
-        stage_q(0)
-        wx_c(0)
-        psx = any_bank([P, 2, P], BF16)
-        xw_t(0, psx)
-        xw_c(0, psx)
         ps = any_bank([P, 2, 2, P], F32)
         stage_cat_t(0, ps)
         stage_cat_c(0, ps)
+        psb = any_bank([P, P], F32)
+        nc.tensor.transpose(psb[:], brow[:].bitcast(F32), ident_f[:])
+        nc.vector.tensor_copy(out=bias[:], in_=psb[:].bitcast(BF16)[:, 0:24])
+        nc.vector.tensor_tensor(out=brz[:], in0=bias[:, 0:8], in1=bias[:, 12:20], op=ALU.add)
+        stage_q(0)
+        x1_bank(0)
 
         pairs = {}
         units = {}
@@ -244,9 +219,6 @@ def tile_wavernncell_pa_t_kernel(tc, x, feat, aux1, h, w_ih, w_hh, b_ih, b_hh, o
             if g == 2:
                 nc.tensor.matmul(gi[:], lhsT=xw[:, c, :], rhs=xmv[:, blk * BB:(blk + 1) * BB, 0], start=False, stop=True)
             return gi
-
-        def e_bank():
-            return psum.tile([P, 2, 2, P], F32, tag="tp", name="ps_e", bufs=2)
 
         def x_term(i, g, t, dst, acc):
             blk, c = divmod(i, 4)
@@ -292,23 +264,13 @@ def tile_wavernncell_pa_t_kernel(tc, x, feat, aux1, h, w_ih, w_hh, b_ih, b_hh, o
                 gi_r = mm_plain(j, 0)
             if lag:
                 gh_n = mm_mx(jn, 2)
-            eb = {}
-            if j == 1:
-                eb["h0"] = e_bank()
-                whh_t(0, 1, eb["h0"])
             if live:
                 gi_z = mm_plain(j, 1)
                 gh_r = mm_mx(j, 0)
-            if j == 1:
-                eb["h1"] = e_bank()
-                whh_t(1, 1, eb["h1"])
-            if live:
-                gh_z = mm_mx(j, 1)
             if lag:
                 gi_n = mm_plain(jn, 2)
-            if j == 1:
-                eb["h2"] = e_bank()
-                whh_t(2, 1, eb["h2"])
+            if live:
+                gh_z = mm_mx(j, 1)
             ps_o = None
             if 0 <= k:
                 ps_o = psum.tile([P, 2, 2, P], F32, tag="tp", name="ps_o", bufs=2)
@@ -320,29 +282,13 @@ def tile_wavernncell_pa_t_kernel(tc, x, feat, aux1, h, w_ih, w_hh, b_ih, b_hh, o
                     stage_h_t(nxt, c, ps_i)
                 else:
                     stage_cat_t(nxt, ps_i)
-            if j == 0:
-                eb["ia"] = e_bank()
-                wih_t(0, 1, eb["ia"], 0)
-                wih_t(1, 1, eb["ia"], 1)
-                eb["ib"] = e_bank()
-                wih_t(2, 1, eb["ib"], 0)
-                stage_h_c(nxt, c, ps_i)
-                wih_c(0, 1, eb["ia"], 0)
-                wih_c(1, 1, eb["ia"], 1)
-            if j == 1:
-                whh_c(0, 1, eb["h0"], False)
-                whh_c(1, 1, eb["h1"], False)
-            if j == 2:
-                psx = psum.tile([P, 2, P], BF16, tag="tp", name="ps_x", bufs=2)
-                xw_t(1, psx)
             if live:
                 if e == 0:
                     pairs[w] = {
                         "a1": ew.tile([P, 2, BB], F32, tag="az1", name="az1"),
+                        "a2": ew.tile([P, 2, BB], F32, tag="az2", name="az2"),
                         "n": ew.tile([P, 2, BB], F32, tag="n", name="n", bufs=3),
                     }
-                    if w < NPAIR - 1:
-                        pairs[w]["a2"] = ew.tile([P, 2, BB], F32, tag="az2", name="az2")
                 pw = pairs[w]
                 a1 = ew.tile([P, BB], F32, tag="a1", name="a1")
                 x_term(j, 0, 0, a1[:], gi_r[:])
@@ -356,39 +302,23 @@ def tile_wavernncell_pa_t_kernel(tc, x, feat, aux1, h, w_ih, w_hh, b_ih, b_hh, o
                 r = ew.tile([P, BB], F32, tag="r", name="r")
                 nc.scalar.activation(out=r[:], in_=a1[:], func=ACT.Sigmoid, bias=brz[:, c:c + 1], scale=1.0)
                 units[j] = r
-                if j == 0:
-                    wih_c(2, 1, eb["ib"], 0)
+            if live and c == 2 and nxt < NBLK:
+                stage_q(nxt)
             if lag:
                 pn = pairs[wn]
                 nc.vector.tensor_tensor(out=v[:], in0=gi_n[:], in1=v[:], op=ALU.add)
                 nc.scalar.activation(out=pn["n"][:, cn % 2, :], in_=v[:], func=ACT.Tanh, bias=bias[:, 8 + cn:9 + cn], scale=1.0)
-                if j == 1:
-                    whh_c(2, 1, eb["h2"], False)
-                if wn == NPAIR - 1:
-                    en = cn % 2
-                    if en == 0:
-                        pn["d"] = ew.tile([P, 2, BB], F32, tag="d", name="d", bufs=3)
-                    ht = staged[jn // 4][0][:].rearrange("p (b t) -> p b t", t=4)[:, :, cn]
-                    eng = nc.gpsimd if en == 0 else nc.vector
-                    eng.tensor_tensor(out=pn["d"][:, en, :], in0=ht, in1=pn["n"][:, en, :], op=ALU.subtract)
-                    eng.tensor_tensor(out=pn["d"][:, en, :], in0=pn["d"][:, en, :], in1=pn["z"][:, en, :], op=ALU.mult)
-                elif cn % 2 == 1:
+                if cn % 2 == 1:
                     pn["d"] = ew.tile([P, 2, BB], F32, tag="d", name="d", bufs=3)
                     un = cn // 2
                     ht = staged[jn // 4][0][:].rearrange("p (b t) -> p t b", t=4)[:, 2 * un:2 * un + 2, :]
-                    nc.gpsimd.tensor_tensor(out=pn["d"][:], in0=ht, in1=pn["n"][:], op=ALU.subtract)
-            if live and w == NPAIR - 1:
-                if e == 0:
-                    pw["z"] = ew.tile([P, 2, BB], F32, tag="z", name="z")
-                az = pw["a1"][:, e, :]
-                nc.vector.scalar_tensor_tensor(out=az, in0=staged[blk][4][:], scalar=wx[:, 1, u, e, 1:2], in1=az, op0=ALU.mult, op1=ALU.add)
-                nc.vector.tensor_tensor(out=az, in0=gh_z[:], in1=az, op=ALU.add)
-                nc.scalar.activation(out=pw["z"][:, e, :], in_=az, func=ACT.Sigmoid, bias=brz[:, 4 + c:5 + c], scale=1.0)
-            elif live:
+                    eng = nc.vector if wn == NPAIR - 1 else nc.gpsimd
+                    eng.tensor_tensor(out=pn["d"][:], in0=ht, in1=pn["n"][:], op=ALU.subtract)
+            if live:
                 x_term(j, 1, 1, pw["a2"][:, e, :], gh_z[:])
                 if e == 1:
                     nc.gpsimd.tensor_tensor(out=pw["a1"][:], in0=pw["a1"][:], in1=pw["a2"][:], op=ALU.add)
-            if j % 2 == 0 and 2 <= j < NUNIT:
+            if j % 2 == 0 and 2 <= j <= NUNIT:
                 wp = w - 1
                 pp = pairs[wp]
                 up = wp % 2
@@ -396,24 +326,15 @@ def tile_wavernncell_pa_t_kernel(tc, x, feat, aux1, h, w_ih, w_hh, b_ih, b_hh, o
                 for ez in range(2):
                     cz = 4 + 2 * up + ez
                     nc.scalar.activation(out=z[:, ez, :], in_=pp["a1"][:, ez, :], func=ACT.Sigmoid, bias=brz[:, cz:cz + 1], scale=1.0)
-                nc.gpsimd.tensor_tensor(out=pp["d"][:], in0=pp["d"][:], in1=z[:], op=ALU.mult)
-            if ps_i is not None and j > 0:
+                eng = nc.vector if wp == NPAIR - 1 else nc.gpsimd
+                eng.tensor_tensor(out=pp["d"][:], in0=pp["d"][:], in1=z[:], op=ALU.mult)
+            if ps_i is not None:
                 if c < 2:
                     stage_h_c(nxt, c, ps_i)
                 else:
                     stage_cat_c(nxt, ps_i)
             if ps_o is not None:
                 out_c(k, ps_o, (not live) and k % 2 == 1)
-            if j == 0:
-                wx_c(1)
-            if j == 1:
-                quant_w(1)
-                quant_w(3)
-            if j == 2:
-                quant_w(5)
-                xw_c(1, psx)
             if live:
-                if c == 2 and nxt < NBLK:
-                    stage_q(nxt)
                 if c == 3 and nxt < NBLK:
                     x1_bank(nxt)

@@ -54,7 +54,7 @@ def tile_wavernncell_pa_t_kernel(tc, x, feat, aux1, h, w_ih, w_hh, b_ih, b_hh, o
         t4 = const.tile([P, 4, P], BF16, name="t4")
         nc.vector.memset(t4[:], 0.0)
         xm = const.tile([P, 2 * B], BF16, name="xm")
-        nc.vector.memset(xm[:], 0.0)
+        nc.vector.memset(xm[:].bitcast(mybir.dt.int32), 0)
 
         whh_sb = const.tile([P, 3, 2, 1024], BF16, name="whh_sb")
         wih_sb = const.tile([P, 3, 2, WROW], BF16, name="wih_sb")
@@ -75,6 +75,7 @@ def tile_wavernncell_pa_t_kernel(tc, x, feat, aux1, h, w_ih, w_hh, b_ih, b_hh, o
         xmv = xm[:].rearrange("p (b i) -> p b i", i=2)
 
         loaded = {}
+        xbs = {}
         staged = {}
         tags = ["tp", "gi", "gh"]
         turn = [0]
@@ -89,9 +90,7 @@ def tile_wavernncell_pa_t_kernel(tc, x, feat, aux1, h, w_ih, w_hh, b_ih, b_hh, o
             cat = ld.tile([P, 4, 256], BF16, tag="cat", name="cat")
             nc.sync.dma_start(out=cat[:, :, 0:128], in_=feat[blk * BB:(blk + 1) * BB, :].rearrange("(s p) k -> p s k", p=P))
             nc.sync.dma_start(out=cat[:, :, 128:256], in_=aux1[blk * BB:(blk + 1) * BB, :].rearrange("(s p) k -> p s k", p=P))
-            xb = ld.tile([P, 2 * BB], BF16, tag="xb", name="xb")
-            nc.sync.dma_start(out=xb[:], in_=xf[blk * 2 * BB:(blk + 1) * 2 * BB].partition_broadcast(P))
-            loaded[blk] = (h_sb, cat, xb)
+            loaded[blk] = (h_sb, cat)
 
         def stage_h_t(blk, half, ps):
             if half == 0:
@@ -116,6 +115,16 @@ def tile_wavernncell_pa_t_kernel(tc, x, feat, aux1, h, w_ih, w_hh, b_ih, b_hh, o
             nc.scalar.copy(out=catt[:], in_=ps[:].rearrange("p a s b -> p (a s b)"))
             staged[blk][3] = catt
 
+        def xb_t(blk, ps):
+            for i in range(2):
+                for s in range(4):
+                    nc.tensor.transpose(ps[:, i, s * P:(s + 1) * P], xs[:, blk * 4 + s, i:i + 1].to_broadcast([P, P]), ident_b[:])
+
+        def xb_c(blk, ps):
+            xb = ld.tile([P, 2, BB], BF16, tag="xb", name="xb")
+            nc.scalar.copy(out=xb[:], in_=ps[:])
+            xbs[blk] = xb
+
         def x1_bank(blk):
             px = psum.tile([P, BB], BF16, tag="px", name="px", bufs=1)
             for s in range(4):
@@ -136,60 +145,90 @@ def tile_wavernncell_pa_t_kernel(tc, x, feat, aux1, h, w_ih, w_hh, b_ih, b_hh, o
                 in_=wgrp[:, gu * 1024:(gu + 1) * 1024],
             )
 
-        def prep_w(u):
-            for g in range(3):
-                gu = g * 2 + u
-                ps = any_bank([P, 2, 2, P], F32)
-                for e in range(2):
-                    for uu in range(2):
-                        lo = e * 256 + uu * P
-                        nc.tensor.transpose(ps[:, uu, e, :], whh_w[:, g, u, lo:lo + P], ident_f[:])
-                dst = wgrp_w[:, gu * 512:(gu + 1) * 512].rearrange("p (e m k) -> p e m k", e=2, k=2)
-                nc.vector.tensor_copy(out=dst, in_=ps[:].rearrange("p k e m -> p e m k"))
-                if g > 0:
-                    quant_w(gu - 2)
-            for g in range(3):
-                gu = g * 2 + u
-                ps2 = any_bank([P, 2, P], F32)
-                for e in range(2):
-                    nc.tensor.transpose(ps2[:, e, :], wih_w[:, g, u, e * 129:e * 129 + P], ident_f[:])
-                src = ps2[:].bitcast(BF16).rearrange("w e (m k) -> w k e m", k=2)
-                nc.scalar.copy(out=wiht[:, :, gu * 2:gu * 2 + 2, :], in_=src)
-            quant_w(4 + u)
+        def whh_t(g, u, ps):
+            for e in range(2):
+                for uu in range(2):
+                    lo = e * 256 + uu * P
+                    nc.tensor.transpose(ps[:, uu, e, :], whh_w[:, g, u, lo:lo + P], ident_f[:])
+
+        def whh_c(g, u, ps, on_vector):
+            gu = g * 2 + u
+            dst = wgrp_w[:, gu * 512:(gu + 1) * 512].rearrange("p (e m k) -> p e m k", e=2, k=2)
+            src = ps[:].rearrange("p k e m -> p e m k")
+            if on_vector:
+                nc.vector.tensor_copy(out=dst, in_=src)
+            else:
+                nc.scalar.copy(out=dst, in_=src)
+
+        def wih_t(g, u, ps, slot):
+            for e in range(2):
+                nc.tensor.transpose(ps[:, slot, e, :], wih_w[:, g, u, e * 129:e * 129 + P], ident_f[:])
+
+        def wih_c(g, u, ps, slot):
+            gu = g * 2 + u
+            src = ps[:, slot, :, :].bitcast(BF16).rearrange("w e (m k) -> w k e m", k=2)
+            nc.scalar.copy(out=wiht[:, :, gu * 2:gu * 2 + 2, :], in_=src)
+
+        def wx_c(u):
             nc.vector.tensor_copy(out=wx[:, :, u, :, :], in_=wih5[:, :, u, :, 256:258])
             nc.vector.tensor_copy(out=t4[:, u * 2:u * 2 + 2, 0:2], in_=wih5[:, 2, u, :, 256:258])
 
-        nc.sync.dma_start(out=whh_sb[:, :, 0, :], in_=whh_v[:, :, 0, :])
-        nc.sync.dma_start(out=wih_sb[:, :, 0, 0:516], in_=wih_v[:, :, 0, :])
-        nc.sync.dma_start(out=whh_sb[:, :, 1, :], in_=whh_v[:, :, 1, :])
-        nc.sync.dma_start(out=wih_sb[:, :, 1, 0:516], in_=wih_v[:, :, 1, :])
-        load(0)
-        nc.sync.dma_start(out=xs[:], in_=x.rearrange("(t p) i -> p t i", p=P))
+        def xw_t(u, ps):
+            for e in range(2):
+                nc.tensor.transpose(ps[:, e, :], t4[:, u * 2 + e, :], ident_b[:])
+
+        def xw_c(u, ps):
+            nc.vector.tensor_copy(out=xw[:, u * 2:u * 2 + 2, :], in_=ps[:])
+
+        xs_v = x.rearrange("(t p) i -> p t i", p=P)
+        nc.sync.dma_start(out=xs[:, 0:8, :], in_=xs_v[:, 0:8, :])
         nc.sync.dma_start(out=brow[0:6, :], in_=b_ih.rearrange("(r c) -> r c", c=256))
         nc.sync.dma_start(out=brow[6:12, :], in_=b_hh.rearrange("(r c) -> r c", c=256))
+        for u in range(2):
+            nc.sync.dma_start(out=whh_sb[:, :, u, :], in_=whh_v[:, :, u, :])
+        for u in range(2):
+            nc.sync.dma_start(out=wih_sb[:, :, u, 0:516], in_=wih_v[:, :, u, :])
+        load(0)
         nc.sync.dma_start(out=xm[0:1, :], in_=xf.unsqueeze(0))
         nc.sync.dma_start(out=xm[1:2, 0:2 * B - 1], in_=xf[1:2 * B].unsqueeze(0))
         load(1)
+        nc.sync.dma_start(out=xs[:, 8:B // P, :], in_=xs_v[:, 8:B // P, :])
 
-        prep_w(0)
-        prep_w(1)
-        psx = any_bank([P, 4, P], BF16)
-        for c in range(4):
-            nc.tensor.transpose(psx[:, c, :], t4[:, c, :], ident_b[:])
-        nc.vector.tensor_copy(out=xw[:], in_=psx[:])
-        for half in range(2):
-            ps = any_bank([P, 2, 2, P], F32)
-            stage_h_t(0, half, ps)
-            stage_h_c(0, half, ps)
-        ps = any_bank([P, 2, 2, P], F32)
-        stage_cat_t(0, ps)
-        stage_cat_c(0, ps)
         psb = any_bank([P, P], F32)
         nc.tensor.transpose(psb[:], brow[:].bitcast(F32), ident_f[:])
         nc.vector.tensor_copy(out=bias[:], in_=psb[:].bitcast(BF16)[:, 0:24])
         nc.vector.tensor_tensor(out=brz[:], in0=bias[:, 0:8], in1=bias[:, 12:20], op=ALU.add)
-        stage_q(0)
+        for blk in range(2):
+            psx = any_bank([P, 2, BB], BF16)
+            xb_t(blk, psx)
+            xb_c(blk, psx)
+        for u in range(2):
+            for g in range(3):
+                ps = any_bank([P, 2, 2, P], F32)
+                whh_t(g, u, ps)
+                whh_c(g, u, ps, True)
+                if g > 0:
+                    quant_w(2 * g - 2 + u)
+            quant_w(4 + u)
+        for u in range(2):
+            for g in range(3):
+                ps = any_bank([P, 2, 2, P], F32)
+                wih_t(g, u, ps, 0)
+                wih_c(g, u, ps, 0)
+            wx_c(u)
+        for u in range(2):
+            psx = any_bank([P, 2, P], BF16)
+            xw_t(u, psx)
+            xw_c(u, psx)
+        for half in range(2):
+            ps = any_bank([P, 2, 2, P], F32)
+            stage_h_t(0, half, ps)
+            stage_h_c(0, half, ps)
         x1_bank(0)
+        ps = any_bank([P, 2, 2, P], F32)
+        stage_cat_t(0, ps)
+        stage_cat_c(0, ps)
+        stage_q(0)
 
         pairs = {}
         units = {}
@@ -222,8 +261,7 @@ def tile_wavernncell_pa_t_kernel(tc, x, feat, aux1, h, w_ih, w_hh, b_ih, b_hh, o
 
         def x_term(i, g, t, dst, acc):
             blk, c = divmod(i, 4)
-            xbv = loaded[blk][2][:].rearrange("p (b i) -> p b i", i=2)
-            nc.vector.scalar_tensor_tensor(out=dst, in0=xbv[:, :, t], scalar=wx[:, g, c // 2, c % 2, t:t + 1], in1=acc, op0=ALU.mult, op1=ALU.add)
+            nc.vector.scalar_tensor_tensor(out=dst, in0=xbs[blk][:, t, :], scalar=wx[:, g, c // 2, c % 2, t:t + 1], in1=acc, op0=ALU.mult, op1=ALU.add)
 
         def out_t(k, ps):
             w, sp = divmod(k, 2)
@@ -282,6 +320,9 @@ def tile_wavernncell_pa_t_kernel(tc, x, feat, aux1, h, w_ih, w_hh, b_ih, b_hh, o
                     stage_h_t(nxt, c, ps_i)
                 else:
                     stage_cat_t(nxt, ps_i)
+            if live and blk + 2 < NBLK and c == 3:
+                ps_i = psum.tile([P, 2, BB], BF16, tag="tp", name="ps_xb", bufs=2)
+                xb_t(blk + 2, ps_i)
             if live:
                 if e == 0:
                     pairs[w] = {
@@ -302,8 +343,6 @@ def tile_wavernncell_pa_t_kernel(tc, x, feat, aux1, h, w_ih, w_hh, b_ih, b_hh, o
                 r = ew.tile([P, BB], F32, tag="r", name="r")
                 nc.scalar.activation(out=r[:], in_=a1[:], func=ACT.Sigmoid, bias=brz[:, c:c + 1], scale=1.0)
                 units[j] = r
-            if live and c == 2 and nxt < NBLK:
-                stage_q(nxt)
             if lag:
                 pn = pairs[wn]
                 nc.vector.tensor_tensor(out=v[:], in0=gi_n[:], in1=v[:], op=ALU.add)
@@ -331,10 +370,14 @@ def tile_wavernncell_pa_t_kernel(tc, x, feat, aux1, h, w_ih, w_hh, b_ih, b_hh, o
             if ps_i is not None:
                 if c < 2:
                     stage_h_c(nxt, c, ps_i)
-                else:
+                elif c == 2:
                     stage_cat_c(nxt, ps_i)
+                else:
+                    xb_c(blk + 2, ps_i)
             if ps_o is not None:
                 out_c(k, ps_o, (not live) and k % 2 == 1)
             if live:
+                if c == 2 and nxt < NBLK:
+                    stage_q(nxt)
                 if c == 3 and nxt < NBLK:
                     x1_bank(nxt)

@@ -54,7 +54,7 @@ def tile_wavernncell_pa_t_kernel(tc, x, feat, aux1, h, w_ih, w_hh, b_ih, b_hh, o
         t4 = const.tile([P, 4, P], BF16, name="t4")
         nc.vector.memset(t4[:], 0.0)
         xm = const.tile([P, 2 * B], BF16, name="xm")
-        nc.vector.memset(xm[:].bitcast(mybir.dt.int32), 0)
+        nc.vector.memset(xm[:], 0.0)
 
         whh_sb = const.tile([P, 3, 2, 1024], BF16, name="whh_sb")
         wih_sb = const.tile([P, 3, 2, WROW], BF16, name="wih_sb")
@@ -75,7 +75,6 @@ def tile_wavernncell_pa_t_kernel(tc, x, feat, aux1, h, w_ih, w_hh, b_ih, b_hh, o
         xmv = xm[:].rearrange("p (b i) -> p b i", i=2)
 
         loaded = {}
-        xbs = {}
         staged = {}
         tags = ["tp", "gi", "gh"]
         turn = [0]
@@ -90,7 +89,9 @@ def tile_wavernncell_pa_t_kernel(tc, x, feat, aux1, h, w_ih, w_hh, b_ih, b_hh, o
             cat = ld.tile([P, 4, 256], BF16, tag="cat", name="cat")
             nc.sync.dma_start(out=cat[:, :, 0:128], in_=feat[blk * BB:(blk + 1) * BB, :].rearrange("(s p) k -> p s k", p=P))
             nc.sync.dma_start(out=cat[:, :, 128:256], in_=aux1[blk * BB:(blk + 1) * BB, :].rearrange("(s p) k -> p s k", p=P))
-            loaded[blk] = (h_sb, cat)
+            xb = ld.tile([P, 2 * BB], BF16, tag="xb", name="xb")
+            nc.sync.dma_start(out=xb[:], in_=xf[blk * 2 * BB:(blk + 1) * 2 * BB].partition_broadcast(P))
+            loaded[blk] = (h_sb, cat, xb)
 
         def stage_h_t(blk, half, ps):
             if half == 0:
@@ -115,16 +116,6 @@ def tile_wavernncell_pa_t_kernel(tc, x, feat, aux1, h, w_ih, w_hh, b_ih, b_hh, o
             nc.scalar.copy(out=catt[:], in_=ps[:].rearrange("p a s b -> p (a s b)"))
             staged[blk][3] = catt
 
-        def xb_t(blk, ps):
-            for i in range(2):
-                for s in range(4):
-                    nc.tensor.transpose(ps[:, i, s * P:(s + 1) * P], xs[:, blk * 4 + s, i:i + 1].to_broadcast([P, P]), ident_b[:])
-
-        def xb_c(blk, ps):
-            xb = ld.tile([P, 2, BB], BF16, tag="xb", name="xb")
-            nc.scalar.copy(out=xb[:], in_=ps[:])
-            xbs[blk] = xb
-
         def x1_bank(blk):
             px = psum.tile([P, BB], BF16, tag="px", name="px", bufs=1)
             for s in range(4):
@@ -145,90 +136,60 @@ def tile_wavernncell_pa_t_kernel(tc, x, feat, aux1, h, w_ih, w_hh, b_ih, b_hh, o
                 in_=wgrp[:, gu * 1024:(gu + 1) * 1024],
             )
 
-        def whh_t(g, u, ps):
-            for e in range(2):
-                for uu in range(2):
-                    lo = e * 256 + uu * P
-                    nc.tensor.transpose(ps[:, uu, e, :], whh_w[:, g, u, lo:lo + P], ident_f[:])
-
-        def whh_c(g, u, ps, on_vector):
-            gu = g * 2 + u
-            dst = wgrp_w[:, gu * 512:(gu + 1) * 512].rearrange("p (e m k) -> p e m k", e=2, k=2)
-            src = ps[:].rearrange("p k e m -> p e m k")
-            if on_vector:
-                nc.vector.tensor_copy(out=dst, in_=src)
-            else:
-                nc.scalar.copy(out=dst, in_=src)
-
-        def wih_t(g, u, ps, slot):
-            for e in range(2):
-                nc.tensor.transpose(ps[:, slot, e, :], wih_w[:, g, u, e * 129:e * 129 + P], ident_f[:])
-
-        def wih_c(g, u, ps, slot):
-            gu = g * 2 + u
-            src = ps[:, slot, :, :].bitcast(BF16).rearrange("w e (m k) -> w k e m", k=2)
-            nc.scalar.copy(out=wiht[:, :, gu * 2:gu * 2 + 2, :], in_=src)
-
-        def wx_c(u):
+        def prep_w(u):
+            for g in range(3):
+                gu = g * 2 + u
+                ps = any_bank([P, 2, 2, P], F32)
+                for e in range(2):
+                    for uu in range(2):
+                        lo = e * 256 + uu * P
+                        nc.tensor.transpose(ps[:, uu, e, :], whh_w[:, g, u, lo:lo + P], ident_f[:])
+                dst = wgrp_w[:, gu * 512:(gu + 1) * 512].rearrange("p (e m k) -> p e m k", e=2, k=2)
+                nc.vector.tensor_copy(out=dst, in_=ps[:].rearrange("p k e m -> p e m k"))
+                if g > 0:
+                    quant_w(gu - 2)
+            for g in range(3):
+                gu = g * 2 + u
+                ps2 = any_bank([P, 2, P], F32)
+                for e in range(2):
+                    nc.tensor.transpose(ps2[:, e, :], wih_w[:, g, u, e * 129:e * 129 + P], ident_f[:])
+                src = ps2[:].bitcast(BF16).rearrange("w e (m k) -> w k e m", k=2)
+                nc.scalar.copy(out=wiht[:, :, gu * 2:gu * 2 + 2, :], in_=src)
+            quant_w(4 + u)
             nc.vector.tensor_copy(out=wx[:, :, u, :, :], in_=wih5[:, :, u, :, 256:258])
             nc.vector.tensor_copy(out=t4[:, u * 2:u * 2 + 2, 0:2], in_=wih5[:, 2, u, :, 256:258])
 
-        def xw_t(u, ps):
-            for e in range(2):
-                nc.tensor.transpose(ps[:, e, :], t4[:, u * 2 + e, :], ident_b[:])
-
-        def xw_c(u, ps):
-            nc.vector.tensor_copy(out=xw[:, u * 2:u * 2 + 2, :], in_=ps[:])
-
-        xs_v = x.rearrange("(t p) i -> p t i", p=P)
-        nc.sync.dma_start(out=xs[:, 0:8, :], in_=xs_v[:, 0:8, :])
+        nc.sync.dma_start(out=whh_sb[:, :, 0, :], in_=whh_v[:, :, 0, :])
+        nc.sync.dma_start(out=wih_sb[:, :, 0, 0:516], in_=wih_v[:, :, 0, :])
+        nc.sync.dma_start(out=whh_sb[:, :, 1, :], in_=whh_v[:, :, 1, :])
+        nc.sync.dma_start(out=wih_sb[:, :, 1, 0:516], in_=wih_v[:, :, 1, :])
+        load(0)
+        nc.sync.dma_start(out=xs[:], in_=x.rearrange("(t p) i -> p t i", p=P))
         nc.sync.dma_start(out=brow[0:6, :], in_=b_ih.rearrange("(r c) -> r c", c=256))
         nc.sync.dma_start(out=brow[6:12, :], in_=b_hh.rearrange("(r c) -> r c", c=256))
-        for u in range(2):
-            nc.sync.dma_start(out=whh_sb[:, :, u, :], in_=whh_v[:, :, u, :])
-        for u in range(2):
-            nc.sync.dma_start(out=wih_sb[:, :, u, 0:516], in_=wih_v[:, :, u, :])
-        load(0)
         nc.sync.dma_start(out=xm[0:1, :], in_=xf.unsqueeze(0))
         nc.sync.dma_start(out=xm[1:2, 0:2 * B - 1], in_=xf[1:2 * B].unsqueeze(0))
         load(1)
-        nc.sync.dma_start(out=xs[:, 8:B // P, :], in_=xs_v[:, 8:B // P, :])
 
-        psb = any_bank([P, P], F32)
-        nc.tensor.transpose(psb[:], brow[:].bitcast(F32), ident_f[:])
-        nc.vector.tensor_copy(out=bias[:], in_=psb[:].bitcast(BF16)[:, 0:24])
-        nc.vector.tensor_tensor(out=brz[:], in0=bias[:, 0:8], in1=bias[:, 12:20], op=ALU.add)
-        for blk in range(2):
-            psx = any_bank([P, 2, BB], BF16)
-            xb_t(blk, psx)
-            xb_c(blk, psx)
-        for u in range(2):
-            for g in range(3):
-                ps = any_bank([P, 2, 2, P], F32)
-                whh_t(g, u, ps)
-                whh_c(g, u, ps, True)
-                if g > 0:
-                    quant_w(2 * g - 2 + u)
-            quant_w(4 + u)
-        for u in range(2):
-            for g in range(3):
-                ps = any_bank([P, 2, 2, P], F32)
-                wih_t(g, u, ps, 0)
-                wih_c(g, u, ps, 0)
-            wx_c(u)
-        for u in range(2):
-            psx = any_bank([P, 2, P], BF16)
-            xw_t(u, psx)
-            xw_c(u, psx)
+        prep_w(0)
+        prep_w(1)
+        psx = any_bank([P, 4, P], BF16)
+        for c in range(4):
+            nc.tensor.transpose(psx[:, c, :], t4[:, c, :], ident_b[:])
+        nc.vector.tensor_copy(out=xw[:], in_=psx[:])
         for half in range(2):
             ps = any_bank([P, 2, 2, P], F32)
             stage_h_t(0, half, ps)
             stage_h_c(0, half, ps)
-        x1_bank(0)
         ps = any_bank([P, 2, 2, P], F32)
         stage_cat_t(0, ps)
         stage_cat_c(0, ps)
+        psb = any_bank([P, P], F32)
+        nc.tensor.transpose(psb[:], brow[:].bitcast(F32), ident_f[:])
+        nc.vector.tensor_copy(out=bias[:], in_=psb[:].bitcast(BF16)[:, 0:24])
+        nc.vector.tensor_tensor(out=brz[:], in0=bias[:, 0:8], in1=bias[:, 12:20], op=ALU.add)
         stage_q(0)
+        x1_bank(0)
 
         pairs = {}
         units = {}
@@ -261,7 +222,8 @@ def tile_wavernncell_pa_t_kernel(tc, x, feat, aux1, h, w_ih, w_hh, b_ih, b_hh, o
 
         def x_term(i, g, t, dst, acc):
             blk, c = divmod(i, 4)
-            nc.vector.scalar_tensor_tensor(out=dst, in0=xbs[blk][:, t, :], scalar=wx[:, g, c // 2, c % 2, t:t + 1], in1=acc, op0=ALU.mult, op1=ALU.add)
+            xbv = loaded[blk][2][:].rearrange("p (b i) -> p b i", i=2)
+            nc.vector.scalar_tensor_tensor(out=dst, in0=xbv[:, :, t], scalar=wx[:, g, c // 2, c % 2, t:t + 1], in1=acc, op0=ALU.mult, op1=ALU.add)
 
         def out_t(k, ps):
             w, sp = divmod(k, 2)
@@ -305,10 +267,10 @@ def tile_wavernncell_pa_t_kernel(tc, x, feat, aux1, h, w_ih, w_hh, b_ih, b_hh, o
             if live:
                 gi_z = mm_plain(j, 1)
                 gh_r = mm_mx(j, 0)
-            if lag:
-                gi_n = mm_plain(jn, 2)
             if live:
                 gh_z = mm_mx(j, 1)
+            if lag:
+                gi_n = mm_plain(jn, 2)
             ps_o = None
             if 0 <= k:
                 ps_o = psum.tile([P, 2, 2, P], F32, tag="tp", name="ps_o", bufs=2)
@@ -320,9 +282,6 @@ def tile_wavernncell_pa_t_kernel(tc, x, feat, aux1, h, w_ih, w_hh, b_ih, b_hh, o
                     stage_h_t(nxt, c, ps_i)
                 else:
                     stage_cat_t(nxt, ps_i)
-            if live and blk + 2 < NBLK and c == 3:
-                ps_i = psum.tile([P, 2, BB], BF16, tag="tp", name="ps_xb", bufs=2)
-                xb_t(blk + 2, ps_i)
             if live:
                 if e == 0:
                     pairs[w] = {
@@ -370,10 +329,8 @@ def tile_wavernncell_pa_t_kernel(tc, x, feat, aux1, h, w_ih, w_hh, b_ih, b_hh, o
             if ps_i is not None:
                 if c < 2:
                     stage_h_c(nxt, c, ps_i)
-                elif c == 2:
-                    stage_cat_c(nxt, ps_i)
                 else:
-                    xb_c(blk + 2, ps_i)
+                    stage_cat_c(nxt, ps_i)
             if ps_o is not None:
                 out_c(k, ps_o, (not live) and k % 2 == 1)
             if live:

@@ -326,13 +326,13 @@ def tile_wavernncell_pa_t_kernel(tc, x, feat, aux1, h, w_ih, w_hh, b_ih, b_hh, o
                     nc.scalar.activation(out=z[:, ez, :], in_=pp["a1"][:, ez, :], func=ACT.Sigmoid, bias=brz[:, cz:cz + 1], scale=1.0)
                 eng = nc.vector if wp == NPAIR - 1 else nc.gpsimd
                 eng.tensor_tensor(out=pp["d"][:], in0=pp["d"][:], in1=z[:], op=ALU.mult)
+            if ps_o is not None:
+                out_c(k, ps_o, (not live) and k % 2 == 1)
             if ps_i is not None:
                 if c < 2:
                     stage_h_c(nxt, c, ps_i)
                 else:
                     stage_cat_c(nxt, ps_i)
-            if ps_o is not None:
-                out_c(k, ps_o, (not live) and k % 2 == 1)
             if live:
                 if c == 2 and nxt < NBLK:
                     stage_q(nxt)

from contextlib import ExitStack

import concourse.mybir as mybir
from concourse.masks import make_identity

F32 = mybir.dt.float32
BF16 = mybir.dt.bfloat16
U32 = mybir.dt.uint32
U8 = mybir.dt.uint8
FP8X4 = mybir.dt.float8_e4m3fn_x4
ALU = mybir.AluOpType
ACT = mybir.ActivationFunctionType

P = 128
B = 4096
H = 512
IN = 258
BB = 512
NBLK = B // BB
NUNIT = NBLK * 4
NPAIR = NUNIT // 2
WROW = 528
FLOPS = 2 * B * 3 * H * (H + IN)
PIN = True
ACC = True
OUT_LAG = 4


def tile_wavernncell_pa_t_kernel(tc, x, feat, aux1, h, w_ih, w_hh, b_ih, b_hh, out):
    nc = tc.nc
    with ExitStack() as ctx:
        const = ctx.enter_context(tc.tile_pool(name="const", bufs=1))
        ld = ctx.enter_context(tc.tile_pool(name="ld", bufs=3))
        stage = ctx.enter_context(tc.tile_pool(name="stage", bufs=2))
        ew = ctx.enter_context(tc.tile_pool(name="ew", bufs=2))
        outp = ctx.enter_context(tc.tile_pool(name="outp", bufs=3))
        psum = ctx.enter_context(tc.psum_pool(name="psum", bufs=3))
        if PIN:
            ctx.enter_context(tc.manual_schedule())

        xf = x.rearrange("b i -> (b i)")
        whh_v = w_hh.rearrange("(g u m e) k -> m g u (e k)", g=3, u=2, m=P, e=2)
        wih_v = w_ih.rearrange("(g u m e) k -> m g u (e k)", g=3, u=2, m=P, e=2)

        warm = const.tile([P, 1], F32, name="warm")
        nc.vector.memset(warm[:], 0.0)
        nc.scalar.activation(out=warm[:], in_=warm[:], func=ACT.Sigmoid)
        ident_f = const.tile([P, P], F32, name="ident_f")
        make_identity(nc, ident_f[:])
        ident_b = const.tile([P, P], BF16, name="ident_b")
        make_identity(nc, ident_b[:])
        brow = const.tile([P, 256], BF16, name="brow")
        nc.vector.memset(brow[:], 0.0)
        t4 = const.tile([P, 4, P], BF16, name="t4")
        nc.vector.memset(t4[:], 0.0)
        xm = const.tile([P, 2 * B], BF16, name="xm")
        nc.vector.memset(xm[:], 0.0)

        whh_sb = const.tile([P, 3, 2, 1024], BF16, name="whh_sb")
        wih_sb = const.tile([P, 3, 2, WROW], BF16, name="wih_sb")
        wgrp = const.tile([P, 12 * 512], BF16, name="wgrp", align_bytes=64)
        wc = const.tile([P, 12 * P], U32, name="wc", align_bytes=64)
        wsc = const.tile([P, 12 * P], U8, name="wsc", align_bytes=64)
        wiht = const.tile([P, 2, 12, P], BF16, name="wiht")
        wx = const.tile([P, 3, 2, 2, 2], F32, name="wx")
        xw = const.tile([P, 4, P], BF16, name="xw")
        bias = const.tile([P, 24], F32, name="bias")
        brz = const.tile([P, 8], F32, name="brz")
        xs = const.tile([P, B // P, 2], BF16, name="xs")

        whh_w = whh_sb[:].bitcast(F32)
        wih_w = wih_sb[:].bitcast(F32)
        wih5 = wih_sb[:, :, :, 0:516].rearrange("m g u (e k) -> m g u e k", e=2)
        wgrp_w = wgrp[:].bitcast(F32)
        xmv = xm[:].rearrange("p (b i) -> p b i", i=2)

        loaded = {}
        staged = {}
        tags = ["tp", "gi", "gh"]
        turn = [0]

        def any_bank(shape, dtype):
            turn[0] += 1
            return psum.tile(shape, dtype, tag=tags[turn[0] % 3], name="ps_pro", bufs=(3 if turn[0] % 3 == 2 else 2))

        def load(blk):
            h_sb = ld.tile([P, 4, H], BF16, tag="h", name="h_sb")
            nc.sync.dma_start(out=h_sb[:], in_=h[blk * BB:(blk + 1) * BB, :].rearrange("(s p) k -> p s k", p=P))
            cat = ld.tile([P, 4, 256], BF16, tag="cat", name="cat")
            nc.sync.dma_start(out=cat[:, :, 0:128], in_=feat[blk * BB:(blk + 1) * BB, :].rearrange("(s p) k -> p s k", p=P))
            nc.sync.dma_start(out=cat[:, :, 128:256], in_=aux1[blk * BB:(blk + 1) * BB, :].rearrange("(s p) k -> p s k", p=P))
            xb = ld.tile([P, 2 * BB], BF16, tag="xb", name="xb")
            nc.sync.dma_start(out=xb[:], in_=xf[blk * 2 * BB:(blk + 1) * 2 * BB].partition_broadcast(P))
            loaded[blk] = (h_sb, cat, xb)

        def stage_h_t(blk, half, ps):
            if half == 0:
                hgrp = stage.tile([P, 4 * BB], BF16, tag="hgrp", name="hgrp", bufs=3, align_bytes=64)
                staged[blk] = [hgrp, None, None, None]
            hw = loaded[blk][0][:].bitcast(F32)
            for s2 in range(2):
                for uu in range(2):
                    nc.tensor.transpose(ps[:, uu, s2, :], hw[:, half * 2 + s2, uu * P:(uu + 1) * P], ident_f[:])

        def stage_h_c(blk, half, ps):
            dst = staged[blk][0][:].bitcast(F32)[:, half * 512:(half + 1) * 512].rearrange("p (b u) -> p b u", u=2)
            nc.scalar.copy(out=dst, in_=ps[:].rearrange("p u s b -> p (s b) u"))

        def stage_cat_t(blk, ps):
            cw = loaded[blk][1][:].bitcast(F32)
            for s in range(4):
                nc.tensor.transpose(ps[:, s // 2, s % 2, :], cw[:, s, :], ident_f[:])

        def stage_cat_c(blk, ps):
            catt = stage.tile([P, BB], F32, tag="catt", name="catt")
            nc.scalar.copy(out=catt[:], in_=ps[:].rearrange("p a s b -> p (a s b)"))
            staged[blk][3] = catt

        def x1_bank(blk):
            px = psum.tile([P, BB], BF16, tag="px", name="px", bufs=1)
            for s in range(4):
                nc.tensor.transpose(px[:, s * P:(s + 1) * P], xs[:, blk * 4 + s, 1:2].to_broadcast([P, P]), ident_b[:])
            staged[blk].append(px)

        def stage_q(blk):
            hc = stage.tile([P, BB], U32, tag="hc", name="hc", align_bytes=64)
            hs = stage.tile([P, BB], U8, tag="hs", name="hs", align_bytes=64)
            nc.vector.quantize_mx(out=hc[:].bitcast(FP8X4), scales=hs[:], in_=staged[blk][0][:])
            staged[blk][1] = hc
            staged[blk][2] = hs

        def quant_w(gu):
            nc.vector.quantize_mx(
                out=wc[:, gu * 256:(gu + 1) * 256].bitcast(FP8X4),
                scales=wsc[:, gu * 256:(gu + 1) * 256],
                in_=wgrp[:, gu * 1024:(gu + 1) * 1024],
            )

        def prep_w(u):
            for g in range(3):
                gu = g * 2 + u
                ps = any_bank([P, 2, 2, P], F32)
                for e in range(2):
                    for uu in range(2):
                        lo = e * 256 + uu * P
                        nc.tensor.transpose(ps[:, uu, e, :], whh_w[:, g, u, lo:lo + P], ident_f[:])
                dst = wgrp_w[:, gu * 512:(gu + 1) * 512].rearrange("p (e m k) -> p e m k", e=2, k=2)
                nc.vector.tensor_copy(out=dst, in_=ps[:].rearrange("p k e m -> p e m k"))
                if g > 0:
                    quant_w(gu - 2)
            for g in range(3):
                gu = g * 2 + u
                ps2 = any_bank([P, 2, P], F32)
                for e in range(2):
                    nc.tensor.transpose(ps2[:, e, :], wih_w[:, g, u, e * 129:e * 129 + P], ident_f[:])
                src = ps2[:].bitcast(BF16).rearrange("w e (m k) -> w k e m", k=2)
                nc.scalar.copy(out=wiht[:, :, gu * 2:gu * 2 + 2, :], in_=src)
            quant_w(4 + u)
            nc.vector.tensor_copy(out=wx[:, :, u, :, :], in_=wih5[:, :, u, :, 256:258])
            nc.vector.tensor_copy(out=t4[:, u * 2:u * 2 + 2, 0:2], in_=wih5[:, 2, u, :, 256:258])

        nc.sync.dma_start(out=whh_sb[:, :, 0, :], in_=whh_v[:, :, 0, :])
        nc.sync.dma_start(out=wih_sb[:, :, 0, 0:516], in_=wih_v[:, :, 0, :])
        nc.sync.dma_start(out=whh_sb[:, :, 1, :], in_=whh_v[:, :, 1, :])
        nc.sync.dma_start(out=wih_sb[:, :, 1, 0:516], in_=wih_v[:, :, 1, :])
        load(0)
        nc.sync.dma_start(out=xs[:], in_=x.rearrange("(t p) i -> p t i", p=P))
        nc.sync.dma_start(out=brow[0:6, :], in_=b_ih.rearrange("(r c) -> r c", c=256))
        nc.sync.dma_start(out=brow[6:12, :], in_=b_hh.rearrange("(r c) -> r c", c=256))
        nc.sync.dma_start(out=xm[0:1, :], in_=xf.unsqueeze(0))
        nc.sync.dma_start(out=xm[1:2, 0:2 * B - 1], in_=xf[1:2 * B].unsqueeze(0))
        load(1)

        prep_w(0)
        prep_w(1)
        psx = any_bank([P, 4, P], BF16)
        for c in range(4):
            nc.tensor.transpose(psx[:, c, :], t4[:, c, :], ident_b[:])
        nc.vector.tensor_copy(out=xw[:], in_=psx[:])
        for half in range(2):
            ps = any_bank([P, 2, 2, P], F32)
            stage_h_t(0, half, ps)
            stage_h_c(0, half, ps)
        ps = any_bank([P, 2, 2, P], F32)
        stage_cat_t(0, ps)
        stage_cat_c(0, ps)
        psb = any_bank([P, P], F32)
        nc.tensor.transpose(psb[:], brow[:].bitcast(F32), ident_f[:])
        nc.vector.tensor_copy(out=bias[:], in_=psb[:].bitcast(BF16)[:, 0:24])
        nc.vector.tensor_tensor(out=brz[:], in0=bias[:, 0:8], in1=bias[:, 12:20], op=ALU.add)
        stage_q(0)
        x1_bank(0)

        pairs = {}
        units = {}

        def mm_mx(i, g):
            blk, c = divmod(i, 4)
            q = g * 4 + c
            gh = psum.tile([P, BB], F32, tag="gh", name="gh")
            nc.tensor.matmul_mx(
                out=gh[:],
                lhsT=wc[:, q * P:(q + 1) * P].bitcast(FP8X4),
                lhsT_scale=wsc[:, q * P:(q + 1) * P],
                rhs=staged[blk][1][:].bitcast(FP8X4),
                rhs_scale=staged[blk][2][:],
                start=True,
                stop=True,
            )
            return gh

        def mm_plain(i, g):
            blk, c = divmod(i, 4)
            q = g * 4 + c
            cb = staged[blk][3][:].bitcast(BF16).rearrange("p (b e) -> p b e", e=2)
            gi = psum.tile([P, BB], F32, tag="gi", name="gi", bufs=2)
            nc.tensor.matmul(gi[:], lhsT=wiht[:, 0, q, :], rhs=cb[:, :, 0], start=True, stop=False)
            nc.tensor.matmul(gi[:], lhsT=wiht[:, 1, q, :], rhs=cb[:, :, 1], start=False, stop=(g < 2))
            if g == 2:
                nc.tensor.matmul(gi[:], lhsT=xw[:, c, :], rhs=xmv[:, blk * BB:(blk + 1) * BB, 0], start=False, stop=True)
            return gi

        def x_term(i, g, t, dst, acc):
            blk, c = divmod(i, 4)
            xbv = loaded[blk][2][:].rearrange("p (b i) -> p b i", i=2)
            nc.vector.scalar_tensor_tensor(out=dst, in0=xbv[:, :, t], scalar=wx[:, g, c // 2, c % 2, t:t + 1], in1=acc, op0=ALU.mult, op1=ALU.add)

        def out_t(k, ps):
            w, sp = divmod(k, 2)
            dd, nn = pairs[w]["d"], pairs[w]["n"]
            for s2 in range(2):
                for e in range(2):
                    lo = (2 * sp + s2) * P
                    nc.tensor.matmul(ps[:, s2, e, :], lhsT=dd[:, e, lo:lo + P], rhs=ident_f[:], is_transpose=True, start=True, stop=False)
                    nc.tensor.matmul(ps[:, s2, e, :], lhsT=nn[:, e, lo:lo + P], rhs=ident_f[:], is_transpose=True, start=False, stop=True)

        def out_c(k, ps, on_vector):
            w, sp = divmod(k, 2)
            blk, u = divmod(w, 2)
            ob = outp.tile([P, 2, 256], F32, tag="ob", name="ob")
            dst = ob[:].rearrange("b s (p e) -> b s p e", e=2)
            src = ps[:].rearrange("b s e p -> b s p e")
            if on_vector:
                nc.vector.tensor_copy(out=dst, in_=src)
            else:
                nc.scalar.copy(out=dst, in_=src)
            r0 = blk * BB + sp * 256
            nc.sync.dma_start(out=out[r0:r0 + 256, u * 256:(u + 1) * 256].rearrange("(s b) j -> b s j", b=P), in_=ob[:])

        for j in range(NUNIT + OUT_LAG):
            blk, c = divmod(j, 4)
            u, e = divmod(c, 2)
            w = j // 2
            live = j < NUNIT
            lag = 1 <= j <= NUNIT
            jn = j - 1
            cn = jn % 4
            wn = jn // 2
            nxt = blk + 1
            k = j - OUT_LAG
            if live:
                if c == 0 and blk + 2 < NBLK:
                    load(blk + 2)
                gi_r = mm_plain(j, 0)
            if lag:
                gh_n = mm_mx(jn, 2)
            if live:
                gi_z = mm_plain(j, 1)
                gh_r = mm_mx(j, 0)
            if live:
                gh_z = mm_mx(j, 1)
            if lag:
                gi_n = mm_plain(jn, 2)
            ps_o = None
            if 0 <= k:
                ps_o = psum.tile([P, 2, 2, P], F32, tag="tp", name="ps_o", bufs=2)
                out_t(k, ps_o)
            ps_i = None
            if live and nxt < NBLK and c < 3:
                ps_i = psum.tile([P, 2, 2, P], F32, tag="tp", name="ps_i", bufs=2)
                if c < 2:
                    stage_h_t(nxt, c, ps_i)
                else:
                    stage_cat_t(nxt, ps_i)
            if live:
                if e == 0:
                    pairs[w] = {
                        "a1": ew.tile([P, 2, BB], F32, tag="az1", name="az1"),
                        "a2": ew.tile([P, 2, BB], F32, tag="az2", name="az2"),
                        "n": ew.tile([P, 2, BB], F32, tag="n", name="n", bufs=3),
                    }
                pw = pairs[w]
                a1 = ew.tile([P, BB], F32, tag="a1", name="a1")
                x_term(j, 0, 0, a1[:], gi_r[:])
            if lag:
                v = ew.tile([P, BB], F32, tag="v", name="v")
                nc.vector.scalar_tensor_tensor(out=v[:], in0=gh_n[:], scalar=bias[:, 20 + cn:21 + cn], in1=units[jn][:], op0=ALU.add, op1=ALU.mult)
            if live:
                nc.vector.scalar_tensor_tensor(out=a1[:], in0=staged[blk][4][:], scalar=wx[:, 0, u, e, 1:2], in1=a1[:], op0=ALU.mult, op1=ALU.add)
                x_term(j, 1, 0, pw["a1"][:, e, :], gi_z[:])
                nc.vector.tensor_tensor(out=a1[:], in0=gh_r[:], in1=a1[:], op=ALU.add)
                r = ew.tile([P, BB], F32, tag="r", name="r")
                nc.scalar.activation(out=r[:], in_=a1[:], func=ACT.Sigmoid, bias=brz[:, c:c + 1], scale=1.0)
                units[j] = r
            if lag:
                pn = pairs[wn]
                nc.vector.tensor_tensor(out=v[:], in0=gi_n[:], in1=v[:], op=ALU.add)
                nc.scalar.activation(out=pn["n"][:, cn % 2, :], in_=v[:], func=ACT.Tanh, bias=bias[:, 8 + cn:9 + cn], scale=1.0)
                if cn % 2 == 1:
                    pn["d"] = ew.tile([P, 2, BB], F32, tag="d", name="d", bufs=3)
                    un = cn // 2
                    ht = staged[jn // 4][0][:].rearrange("p (b t) -> p t b", t=4)[:, 2 * un:2 * un + 2, :]
                    eng = nc.vector if wn == NPAIR - 1 else nc.gpsimd
                    eng.tensor_tensor(out=pn["d"][:], in0=ht, in1=pn["n"][:], op=ALU.subtract)
            if live:
                x_term(j, 1, 1, pw["a2"][:, e, :], gh_z[:])
                if e == 1:
                    nc.gpsimd.tensor_tensor(out=pw["a1"][:], in0=pw["a1"][:], in1=pw["a2"][:], op=ALU.add)
            if j % 2 == 0 and 2 <= j <= NUNIT:
                wp = w - 1
                pp = pairs[wp]
                up = wp % 2
                z = ew.tile([P, 2, BB], F32, tag="z", name="z")
                for ez in range(2):
                    cz = 4 + 2 * up + ez
                    nc.scalar.activation(out=z[:, ez, :], in_=pp["a1"][:, ez, :], func=ACT.Sigmoid, bias=brz[:, cz:cz + 1], scale=1.0)
                eng = nc.vector if wp == NPAIR - 1 else nc.gpsimd
                eng.tensor_tensor(out=pp["d"][:], in0=pp["d"][:], in1=z[:], op=ALU.mult)
            if ps_o is not None:
                out_c(k, ps_o, (not live) and k % 2 == 1)
            if ps_i is not None:
                if c < 2:
                    stage_h_c(nxt, c, ps_i)
                else:
                    stage_cat_c(nxt, ps_i)
            if live:
                if c == 2 and nxt < NBLK:
                    stage_q(nxt)
                if c == 3 and nxt < NBLK:
                    x1_bank(nxt)
